import numpy as np
import ml_dtypes


def mxq(x, axis, fmt="e4m3"):
    dtype, down = {"e4m3": (ml_dtypes.float8_e4m3fn, 7), "e5m2": (ml_dtypes.float8_e5m2, 14)}[fmt]
    v = np.moveaxis(np.asarray(x, np.float32).astype(ml_dtypes.bfloat16).astype(np.float64), axis, -1)
    blocks = v.reshape(v.shape[:-1] + (-1, 32))
    amax = np.abs(blocks).max(-1, keepdims=True)
    byte = np.maximum(np.where(amax > 0, np.frexp(amax)[1] - 1 + 127, 0) - down, 1)
    scale = np.exp2(byte - 127.0)
    codes = (blocks / scale).astype(np.float32).astype(dtype).astype(np.float64)
    return np.moveaxis((codes * scale).reshape(v.shape), -1, axis)


WIDE = False


def mx_kscale(k):
    if not WIDE:
        return np.ones(k)
    levels = np.array([10, -10, 5, -5, 0])
    a = np.random.permutation(np.resize(levels, k // 512 * 4)).reshape(k // 512, 4)
    idx = np.arange(k)
    return np.exp2(a[idx // 512, idx % 128 // 32])


BF16 = ml_dtypes.bfloat16


def bf(x):
    return np.asarray(x, np.float32).astype(BF16)


def f64(x):
    return np.asarray(x).astype(np.float64)


B, N_OUT, SO, SI, NV, NC, N_PHI, N_DIST, N_SIGMA = 4, 32, 16, 32, 1, 32, 16, 16, 2
DIST_UNIT = 2.0
MIN_SIGMA = 1e-10


def sigmoid(v):
    return 1.0 / (1.0 + np.exp(-v))


def setup_inputs():
    n_in = N_OUT * SO * SI
    a = 2.0 * np.maximum(np.log2(mx_kscale(SO * SI)), 0.0)
    x = bf(np.random.standard_normal((B, n_in, 1, NV, NC)) * 2.0 * np.tile(2.0 ** a, N_OUT)[None, :, None, None, None])
    ux = np.random.uniform(-DIST_UNIT, DIST_UNIT, (1, N_OUT, SO, SI))
    uy = np.random.uniform(-DIST_UNIT, DIST_UNIT, (1, N_OUT, SO, SI))
    phis = bf(np.linspace(-np.pi, np.pi, N_PHI + 1)[:-1] + 0.05 * np.random.standard_normal(N_PHI))
    d = np.arange(1, 2 * N_DIST, 2) / (N_DIST * 2)
    dists_param = bf(-np.log(1.0 / d - 1.0) + 0.1 * np.random.standard_normal(N_DIST))
    s = 0.1 * np.arange(1, N_SIGMA + 1)
    sigma_param = bf(-np.log(1.0 / s - 1.0) + 0.1 * np.random.standard_normal(N_SIGMA))
    dmax = (DIST_UNIT * sigmoid(f64(dists_param))).max()
    smax = (DIST_UNIT * sigmoid(f64(sigma_param))).max()
    A = a.reshape(1, 1, SO, SI)
    R = dmax + smax * np.sqrt(2.0 * np.log(2.0) * A)
    r = np.hypot(ux, uy)
    coords_x = bf(np.where(A > 0, ux / r * R, ux))
    coords_y = bf(np.where(A > 0, uy / r * R, uy))
    return {"x": x, "coords_x": coords_x, "coords_y": coords_y, "phis": phis, "dists_param": dists_param, "sigma_param": sigma_param}


def reference(x, coords_x, coords_y, phis, dists_param, sigma_param):
    x, coords_x, coords_y = f64(x), f64(coords_x), f64(coords_y)
    phis, dists_param, sigma_param = f64(phis), f64(dists_param), f64(sigma_param)
    b = x.shape[0]
    nv, nc = x.shape[-2], x.shape[-1]
    n_out, so, si = coords_x.shape[1], coords_x.shape[2], coords_x.shape[3]
    n_p, n_d, n_s = phis.shape[0], dists_param.shape[0], sigma_param.shape[0]

    dists = DIST_UNIT * sigmoid(dists_param)
    mu_x = np.cos(phis)[:, None] * dists[None, :]
    mu_y = np.sin(phis)[:, None] * dists[None, :]
    sigma = np.maximum(DIST_UNIT * sigmoid(sigma_param), MIN_SIGMA)

    dx = coords_x[0][..., None, None] - mu_x
    dy = coords_y[0][..., None, None] - mu_y
    w = np.exp(-0.5 * (dx * dx + dy * dy)[..., None] / (sigma * sigma))
    w = w / (w.sum(axis=(1, 2), keepdims=True) + 1e-20)

    wq = mxq(w.reshape(n_out, so * si, n_p * n_d * n_s), 1, "e4m3")
    xq = mxq(x.reshape(b, n_out, so * si, nv, nc), 2, "e4m3")
    out = wq.transpose(0, 2, 1)[None, :, None] @ xq.transpose(0, 1, 3, 2, 4)
    return out.reshape(b, n_out, nv, n_p, n_d, n_s, nc)

@@ -1,0 +1,303 @@
+import math
+from contextlib import ExitStack
+
+import concourse.bass as bass
+import concourse.mybir as mybir
+import concourse.tile as tile
+from concourse.masks import make_identity
+
+F32 = mybir.dt.float32
+BF16 = mybir.dt.bfloat16
+I32 = mybir.dt.int32
+U32 = mybir.dt.uint32
+U8 = mybir.dt.uint8
+FP8X4 = mybir.dt.float8_e4m3fn_x4
+ALU = mybir.AluOpType
+ACTF = mybir.ActivationFunctionType
+
+P = 128
+FLOPS = 2 * 32 * 512 * 512 * 128
+
+TWO_PI_HI = 6.28125
+TWO_PI_LO = 2.0 * math.pi - 6.28125
+PI_F32 = 3.1415927410125732
+
+VECTOR_BANKS = ((1, 1),)
+
+
+def tile_polnormal_nolayer_kernel(tc, x, coords_x, coords_y, phis, dists_param, sigma_param, out):
+    nc = tc.nc
+    V = nc.vector
+    S = nc.scalar
+    T = nc.tensor
+    with ExitStack() as ctx:
+        const = ctx.enter_context(tc.tile_pool(name="const", bufs=1))
+        tmp = ctx.enter_context(tc.tile_pool(name="tmp", bufs=2))
+        zp = ctx.enter_context(tc.tile_pool(name="zp", bufs=6))
+        gp = ctx.enter_context(tc.tile_pool(name="gp", bufs=8))
+        wp = ctx.enter_context(tc.tile_pool(name="wp", bufs=8))
+        sp = ctx.enter_context(tc.tile_pool(name="sp", bufs=3))
+        xgp = ctx.enter_context(tc.tile_pool(name="xgp", bufs=2))
+        cp = ctx.enter_context(tc.tile_pool(name="cp", bufs=4))
+        op = ctx.enter_context(tc.tile_pool(name="op", bufs=4))
+        ptp = ctx.enter_context(tc.psum_pool(name="ptp", bufs=5))
+        pacc = ctx.enter_context(tc.psum_pool(name="pacc", bufs=2))
+        pss = ctx.enter_context(tc.psum_pool(name="pss", bufs=1))
+        ctx.enter_context(nc.allow_non_contiguous_dma(reason="rows of 256 and 512 bytes"))
+
+        cn = const.tile([P, 512], BF16)
+        V.memset(cn[:].bitcast(I32), 0)
+        nc.sync.dma_start(out=cn[0:32, :], in_=coords_x.rearrange("a o i j -> (a o) (i j)"))
+        nc.sync.dma_start(out=cn[32:64, :], in_=coords_y.rearrange("a o i j -> (a o) (i j)"))
+        phr = const.tile([P, 16], BF16)
+        nc.sync.dma_start(out=phr[:], in_=phis.partition_broadcast(P))
+        dpr = const.tile([P, 16], BF16)
+        nc.sync.dma_start(out=dpr[:], in_=dists_param.partition_broadcast(P))
+        spr = const.tile([P, 2], BF16)
+        nc.sync.dma_start(out=spr[:], in_=sigma_param.partition_broadcast(P))
+        xr = const.tile([P, 4, 32, 128], BF16)
+        for b in range(4):
+            nc.sync.dma_start(
+                out=xr[:, b], in_=x[b].rearrange("(o q t) a v c -> q o (t a v c)", o=32, q=P, t=4)
+            )
+
+        ident = const.tile([P, P], F32)
+        make_identity(nc, ident[:])
+        identb = const.tile([P, P], BF16)
+        make_identity(nc, identb[:])
+
+        pair = const.tile([P, 64, 2], F32)
+        idv = ident[:].rearrange("q (c e) -> q c e", e=2)
+        V.tensor_tensor(
+            out=pair[:],
+            in0=idv[:, :, 0:1].to_broadcast([P, 64, 2]),
+            in1=idv[:, :, 1:2].to_broadcast([P, 64, 2]),
+            op=ALU.add,
+        )
+
+        thd = const.tile([P, 16], F32)
+        S.activation(out=thd[:], in_=dpr[:], func=ACTF.Tanh, scale=0.5)
+        ths = const.tile([P, 2], F32)
+        S.activation(out=ths[:], in_=spr[:], func=ACTF.Tanh, scale=0.5)
+        dm2 = const.tile([P, 16], F32)
+        V.tensor_scalar(out=dm2[:], in0=thd[:], scalar1=1.0, scalar2=-2.0, op0=ALU.add, op1=ALU.mult)
+        dd = const.tile([P, 16], F32)
+        V.tensor_scalar(out=dd[:], in0=thd[:], scalar1=1.0, scalar2=None, op0=ALU.add)
+        dsq = const.tile([P, 16], F32)
+        V.tensor_tensor(out=dsq[:], in0=dd[:], in1=dd[:], op=ALU.mult)
+        sg = const.tile([P, 2], F32)
+        V.tensor_scalar(out=sg[:], in0=ths[:], scalar1=1.0, scalar2=1e-10, op0=ALU.add, op1=ALU.max)
+        sg2 = const.tile([P, 2], F32)
+        V.tensor_tensor(out=sg2[:], in0=sg[:], in1=sg[:], op=ALU.mult)
+        rsg = const.tile([P, 2], F32)
+        V.reciprocal(out=rsg[:], in_=sg2[:])
+        nha = const.tile([P, 2], F32)
+        V.tensor_scalar(out=nha[:], in0=rsg[:], scalar1=-0.5, scalar2=None, op0=ALU.mult)
+        bias = const.tile([P, 2, 16], F32)
+        for s in range(2):
+            V.tensor_scalar(out=bias[:, s, :], in0=dsq[:], scalar1=nha[:, s : s + 1], scalar2=None, op0=ALU.mult)
+
+        phf = const.tile([P, 16], F32)
+        V.tensor_copy(out=phf[:], in_=phr[:])
+        qi = const.tile([P, 16], I32)
+        V.tensor_scalar(out=qi[:], in0=phf[:], scalar1=1.0 / (2.0 * math.pi), scalar2=None, op0=ALU.mult)
+        qf = const.tile([P, 16], F32)
+        V.tensor_copy(out=qf[:], in_=qi[:])
+        p1 = const.tile([P, 16], F32)
+        V.scalar_tensor_tensor(out=p1[:], in0=qf[:], scalar=-TWO_PI_HI, in1=phf[:], op0=ALU.mult, op1=ALU.add)
+        p2 = const.tile([P, 16], F32)
+        V.scalar_tensor_tensor(out=p2[:], in0=qf[:], scalar=-TWO_PI_LO, in1=p1[:], op0=ALU.mult, op1=ALU.add)
+        over = const.tile([P, 16], F32)
+        V.tensor_scalar(out=over[:], in0=p2[:], scalar1=PI_F32, scalar2=-1.0, op0=ALU.is_gt, op1=ALU.mult)
+        turn = const.tile([P, 16], F32)
+        V.scalar_tensor_tensor(out=turn[:], in0=p2[:], scalar=-PI_F32, in1=over[:], op0=ALU.is_lt, op1=ALU.add)
+        p3 = const.tile([P, 16], F32)
+        V.scalar_tensor_tensor(out=p3[:], in0=turn[:], scalar=TWO_PI_HI, in1=p2[:], op0=ALU.mult, op1=ALU.add)
+        ang = const.tile([P, 2, 16], F32)
+        V.scalar_tensor_tensor(out=ang[:, 0, :], in0=turn[:], scalar=TWO_PI_LO, in1=p3[:], op0=ALU.mult, op1=ALU.add)
+        aab = const.tile([P, 16], F32)
+        V.scalar_tensor_tensor(out=aab[:], in0=ang[:, 0, :], scalar=-1.0, in1=ang[:, 0, :], op0=ALU.mult, op1=ALU.max)
+        V.tensor_scalar(out=ang[:, 1, :], in0=aab[:], scalar1=-1.0, scalar2=0.5 * math.pi, op0=ALU.mult, op1=ALU.add)
+        cs = const.tile([P, 2, 16], F32)
+        S.activation(out=cs[:], in_=ang[:], func=ACTF.Sin)
+
+        cn2 = const.tile([P, 4, P], BF16)
+        V.tensor_copy(out=cn2[:], in_=cn[:].rearrange("r (q t) -> r t q", t=4))
+        pc = ptp.tile([P, 4, P], BF16, tag="tp")
+        for t in range(4):
+            T.transpose(out=pc[:, t, :], in_=cn2[:, t, :], identity=identb[:])
+        cq = const.tile([P, 2, 8, 2, 4, 2], F32)
+        for xy in range(2):
+            V.tensor_copy(
+                out=cq[:, xy],
+                in_=pc[:, :, 32 * xy : 32 * xy + 32].rearrange("q (u e) (g n) -> q g u n e", e=2, n=4),
+            )
+        sq = const.tile([P, 2, P], F32)
+        cqf = cq[:].rearrange("q a g u n e -> q a (g u n e)")
+        V.tensor_tensor(out=sq[:], in0=cqf, in1=cqf, op=ALU.mult)
+        r2q = const.tile([P, P], F32)
+        V.tensor_tensor(out=r2q[:], in0=sq[:, 0, :], in1=sq[:, 1, :], op=ALU.add)
+
+        ta = const.tile([P, 2048], F32)
+        ra = const.tile([P, 2048], F32)
+        shape4 = [P, 16, 16, 2]
+
+        def tables(sgi):
+            def spread(flat):
+                return flat.rearrange("q (c e) -> q c e", e=2).unsqueeze(2).to_broadcast(shape4)
+
+            def trig(row):
+                return cs[:, row, :].unsqueeze(1).unsqueeze(3).to_broadcast(shape4)
+
+            cols = slice(32 * sgi, 32 * sgi + 32)
+            tx = tmp.tile(shape4, F32)
+            V.tensor_tensor(out=tx[:], in0=spread(cqf[:, 0, cols]), in1=trig(1), op=ALU.mult)
+            ty = tmp.tile(shape4, F32)
+            V.tensor_tensor(out=ty[:], in0=spread(cqf[:, 1, cols]), in1=trig(0), op=ALU.mult)
+            tq = tmp.tile(shape4, F32)
+            V.tensor_tensor(out=tq[:], in0=tx[:], in1=ty[:], op=ALU.add)
+            rq = tmp.tile(shape4, F32)
+            V.tensor_copy(out=rq[:], in_=spread(r2q[:, cols]))
+            for src, dst in ((tq, ta), (rq, ra)):
+                flat = src[:].rearrange("q c p e -> q (c p e)")
+                pt = ptp.tile([P, 512], F32, tag="tp")
+                for blk in range(4):
+                    T.transpose(
+                        out=pt[:, blk * P : (blk + 1) * P], in_=flat[:, blk * P : (blk + 1) * P], identity=ident[:]
+                    )
+                S.copy(out=dst[:, 512 * sgi : 512 * sgi + 512], in_=pt[:])
+
+        xc = const.tile([P, 4096], U32, align_bytes=64)
+        xs = const.tile([P, 4096], U8, align_bytes=64)
+
+        def x_stage(sgi):
+            xg = xgp.tile([P, 8, 4, 32, 4], BF16, align_bytes=64)
+            for b in range(4):
+                V.tensor_copy(
+                    out=xg[:, :, b, :, :],
+                    in_=xr[:, b, 8 * sgi : 8 * sgi + 8, :].rearrange("q o (t c) -> q o c t", t=4),
+                )
+            cols = slice(1024 * sgi, 1024 * sgi + 1024)
+            V.quantize_mx(
+                out=xc[:, cols].bitcast(FP8X4), scales=xs[:, cols], in_=xg[:].rearrange("q o b c t -> q (o b c t)")
+            )
+
+        wg = [const.tile([P, 8192], BF16, align_bytes=64, name="wg%d" % gh) for gh in range(2)]
+        live = {}
+
+        def stage_a(qq):
+            sgi, a = divmod(qq, 4)
+            ssum = sp.tile([P, 16], F32)
+            gs = []
+            for dq in range(4):
+                d = 4 * a + dq
+                cols = slice(512 * sgi, 512 * sgi + 512)
+                z = zp.tile([P, 512], F32)
+                V.scalar_tensor_tensor(
+                    out=z[:], in0=ta[:, cols], scalar=dm2[:, d : d + 1], in1=ra[:, cols], op0=ALU.mult, op1=ALU.add
+                )
+                g = gp.tile([P, 2, 2, 256], F32)
+                for gh in range(2):
+                    for s in range(2):
+                        c = dq * 4 + gh * 2 + s
+                        S.activation(
+                            out=g[:, gh, s, :],
+                            in_=z[:, 256 * gh : 256 * gh + 256],
+                            func=ACTF.Exp,
+                            bias=bias[:, s, d : d + 1],
+                            scale=nha[:, s : s + 1],
+                            accum_out=ssum[:, c : c + 1],
+                        )
+                gs.append(g)
+            live[qq] = (ssum, gs)
+
+        def stage_b(qq):
+            ssum, gs = live[qq]
+            ps = pss.tile([P, 16], F32)
+            T.matmul(out=ps[:], lhsT=pair[:].rearrange("q c e -> q (c e)"), rhs=ssum[:], start=True, stop=True)
+            tot = sp.tile([P, 16], F32)
+            V.tensor_scalar(out=tot[:], in0=ps[:], scalar1=1e-20, scalar2=None, op0=ALU.add)
+            inv = sp.tile([P, 16], F32)
+            V.reciprocal(out=inv[:], in_=tot[:])
+            ws = []
+            for dq in range(4):
+                w = wp.tile([P, 2, 2, 256], BF16)
+                for gh in range(2):
+                    for s in range(2):
+                        c = dq * 4 + gh * 2 + s
+                        V.tensor_scalar(
+                            out=w[:, gh, s, :], in0=gs[dq][:, gh, s, :], scalar1=inv[:, c : c + 1], scalar2=None,
+                            op0=ALU.mult,
+                        )
+                ws.append(w)
+            banks = {}
+            for gh in range(2):
+                for dlo in range(2):
+                    tp = ptp.tile([P, 2, 2, 2, P], BF16, tag="tp")
+                    for s in range(2):
+                        for h in range(2):
+                            for u in range(2):
+                                T.transpose(
+                                    out=tp[:, s, h, u, :],
+                                    in_=ws[2 * h + dlo][:, gh, s, P * u : P * u + P],
+                                    identity=identb[:],
+                                )
+                    banks[(gh, dlo)] = tp
+            live[qq] = banks
+
+        def stage_c(qq):
+            a = qq % 4
+            banks = live[qq]
+            for gh in range(2):
+                wv = wg[gh][:].rearrange("q (n i p a r e) -> q n i p a r e", n=4, i=4, p=16, a=4, r=4, e=2)
+                for dlo in range(2):
+                    tp = banks[(gh, dlo)]
+                    for s in range(2):
+                        dst = wv[:, :, 2 * dlo + s, :, a, :, :]
+                        src = tp[:, s].rearrange("q h u (n p e) -> q n p (h u) e", n=4, p=16, e=2)
+                        if (gh, dlo) in VECTOR_BANKS:
+                            V.tensor_copy(out=dst, in_=src)
+                        else:
+                            S.copy(out=dst, in_=src)
+
+        def stage_d(sgi):
+            for gh in range(2):
+                for n in range(4):
+                    o = 8 * sgi + 4 * gh + n
+                    wc = cp.tile([P, 512], U32, align_bytes=64)
+                    wsc = cp.tile([P, 512], U8, align_bytes=64)
+                    V.quantize_mx(out=wc[:].bitcast(FP8X4), scales=wsc[:], in_=wg[gh][:, 2048 * n : 2048 * n + 2048])
+                    acc = pacc.tile([P, 512], F32)
+                    for i in range(4):
+                        mc = slice(P * i, P * i + P)
+                        oc = slice(P * o, P * o + P)
+                        T.matmul_mx(
+                            out=acc[:, mc],
+                            lhsT=wc[:, mc].bitcast(FP8X4),
+                            lhsT_scale=wsc[:, mc],
+                            rhs=xc[:, oc].bitcast(FP8X4),
+                            rhs_scale=xs[:, oc],
+                            start=True,
+                            stop=True,
+                        )
+                    osb = op.tile([P, 4, 4, 32], F32)
+                    S.copy(out=osb[:], in_=acc[:].rearrange("q (i b c) -> q b i c", i=4, b=4))
+                    nc.sync.dma_start(
+                        out=out[:, o].rearrange("b v p (h l) s c -> (v p h) b (l s c)", l=2),
+                        in_=osb[:].rearrange("q b i c -> q b (i c)"),
+                    )
+
+        tables(0)
+        for step in range(18):
+            if step < 16:
+                if step % 4 == 1 and step // 4 < 3:
+                    tables(step // 4 + 1)
+                if step % 4 == 2:
+                    x_stage(step // 4)
+                stage_a(step)
+            if step >= 2:
+                stage_c(step - 2)
+                if (step - 2) % 4 == 3:
+                    stage_d((step - 2) // 4)
+            if 1 <= step <= 16:
+                stage_b(step - 1)

@@ -22,7 +22,7 @@ TWO_PI_HI = 6.28125
 TWO_PI_LO = 2.0 * math.pi - 6.28125
 PI_F32 = 3.1415927410125732
 
-VECTOR_BANKS = ((1, 1),)
+N_PAIRS = 32
 
 
 def tile_polnormal_nolayer_kernel(tc, x, coords_x, coords_y, phis, dists_param, sigma_param, out):
@@ -33,16 +33,17 @@ def tile_polnormal_nolayer_kernel(tc, x, coords_x, coords_y, phis, dists_param, 
     with ExitStack() as ctx:
         const = ctx.enter_context(tc.tile_pool(name="const", bufs=1))
         tmp = ctx.enter_context(tc.tile_pool(name="tmp", bufs=2))
-        zp = ctx.enter_context(tc.tile_pool(name="zp", bufs=6))
-        gp = ctx.enter_context(tc.tile_pool(name="gp", bufs=8))
+        tqp = ctx.enter_context(tc.tile_pool(name="tqp", bufs=2))
+        yp = ctx.enter_context(tc.tile_pool(name="yp", bufs=4))
+        gp = ctx.enter_context(tc.tile_pool(name="gp", bufs=10))
         wp = ctx.enter_context(tc.tile_pool(name="wp", bufs=8))
         sp = ctx.enter_context(tc.tile_pool(name="sp", bufs=3))
         xgp = ctx.enter_context(tc.tile_pool(name="xgp", bufs=2))
-        cp = ctx.enter_context(tc.tile_pool(name="cp", bufs=4))
+        cp = ctx.enter_context(tc.tile_pool(name="cp", bufs=3))
         op = ctx.enter_context(tc.tile_pool(name="op", bufs=4))
-        ptp = ctx.enter_context(tc.psum_pool(name="ptp", bufs=5))
+        pz = ctx.enter_context(tc.psum_pool(name="pz", bufs=4))
+        ptp = ctx.enter_context(tc.psum_pool(name="ptp", bufs=2))
         pacc = ctx.enter_context(tc.psum_pool(name="pacc", bufs=2))
-        pss = ctx.enter_context(tc.psum_pool(name="pss", bufs=1))
         ctx.enter_context(nc.allow_non_contiguous_dma(reason="rows of 256 and 512 bytes"))
 
         cn = const.tile([P, 512], BF16)
@@ -65,15 +66,6 @@ def tile_polnormal_nolayer_kernel(tc, x, coords_x, coords_y, phis, dists_param, 
         make_identity(nc, ident[:])
         identb = const.tile([P, P], BF16)
         make_identity(nc, identb[:])
-
-        pair = const.tile([P, 64, 2], F32)
-        idv = ident[:].rearrange("q (c e) -> q c e", e=2)
-        V.tensor_tensor(
-            out=pair[:],
-            in0=idv[:, :, 0:1].to_broadcast([P, 64, 2]),
-            in1=idv[:, :, 1:2].to_broadcast([P, 64, 2]),
-            op=ALU.add,
-        )
 
         thd = const.tile([P, 16], F32)
         S.activation(out=thd[:], in_=dpr[:], func=ACTF.Tanh, scale=0.5)
@@ -126,178 +118,207 @@ def tile_polnormal_nolayer_kernel(tc, x, coords_x, coords_y, phis, dists_param, 
         pc = ptp.tile([P, 4, P], BF16, tag="tp")
         for t in range(4):
             T.transpose(out=pc[:, t, :], in_=cn2[:, t, :], identity=identb[:])
-        cq = const.tile([P, 2, 8, 2, 4, 2], F32)
-        for xy in range(2):
-            V.tensor_copy(
-                out=cq[:, xy],
-                in_=pc[:, :, 32 * xy : 32 * xy + 32].rearrange("q (u e) (g n) -> q g u n e", e=2, n=4),
-            )
+        cq = const.tile([P, 2, 4, 32], F32)
+        V.tensor_copy(out=cq[:], in_=pc[:, :, 0:64].rearrange("q t (a o) -> q a t o", a=2))
         sq = const.tile([P, 2, P], F32)
-        cqf = cq[:].rearrange("q a g u n e -> q a (g u n e)")
+        cqf = cq[:].rearrange("q a t o -> q a (t o)")
         V.tensor_tensor(out=sq[:], in0=cqf, in1=cqf, op=ALU.mult)
-        r2q = const.tile([P, P], F32)
-        V.tensor_tensor(out=r2q[:], in0=sq[:, 0, :], in1=sq[:, 1, :], op=ALU.add)
+        r2q = const.tile([P, 4, 32], F32)
+        V.tensor_tensor(out=r2q[:].rearrange("q t o -> q (t o)"), in0=sq[:, 0, :], in1=sq[:, 1, :], op=ALU.add)
 
-        ta = const.tile([P, 2048], F32)
-        ra = const.tile([P, 2048], F32)
-        shape4 = [P, 16, 16, 2]
+        shape4 = [P, 4, 8, 16]
+        tabs = {}
 
-        def tables(sgi):
-            def spread(flat):
-                return flat.rearrange("q (c e) -> q c e", e=2).unsqueeze(2).to_broadcast(shape4)
+        def tables(grp):
+            nodes = slice(8 * grp, 8 * grp + 8)
 
             def trig(row):
-                return cs[:, row, :].unsqueeze(1).unsqueeze(3).to_broadcast(shape4)
+                return cs[:, row, :].unsqueeze(1).unsqueeze(1).to_broadcast(shape4)
 
-            cols = slice(32 * sgi, 32 * sgi + 32)
             tx = tmp.tile(shape4, F32)
-            V.tensor_tensor(out=tx[:], in0=spread(cqf[:, 0, cols]), in1=trig(1), op=ALU.mult)
+            V.tensor_tensor(out=tx[:], in0=cq[:, 0, :, nodes].unsqueeze(3).to_broadcast(shape4), in1=trig(1), op=ALU.mult)
             ty = tmp.tile(shape4, F32)
-            V.tensor_tensor(out=ty[:], in0=spread(cqf[:, 1, cols]), in1=trig(0), op=ALU.mult)
-            tq = tmp.tile(shape4, F32)
+            V.tensor_tensor(out=ty[:], in0=cq[:, 1, :, nodes].unsqueeze(3).to_broadcast(shape4), in1=trig(0), op=ALU.mult)
+            tq = tqp.tile(shape4, F32)
             V.tensor_tensor(out=tq[:], in0=tx[:], in1=ty[:], op=ALU.add)
-            rq = tmp.tile(shape4, F32)
-            V.tensor_copy(out=rq[:], in_=spread(r2q[:, cols]))
-            for src, dst in ((tq, ta), (rq, ra)):
-                flat = src[:].rearrange("q c p e -> q (c p e)")
-                pt = ptp.tile([P, 512], F32, tag="tp")
-                for blk in range(4):
-                    T.transpose(
-                        out=pt[:, blk * P : (blk + 1) * P], in_=flat[:, blk * P : (blk + 1) * P], identity=ident[:]
-                    )
-                S.copy(out=dst[:, 512 * sgi : 512 * sgi + 512], in_=pt[:])
+            rq = tqp.tile(shape4, F32)
+            V.tensor_copy(out=rq[:], in_=r2q[:, :, nodes].unsqueeze(3).to_broadcast(shape4))
+            tabs[grp] = (tq, rq)
 
         xc = const.tile([P, 4096], U32, align_bytes=64)
         xs = const.tile([P, 4096], U8, align_bytes=64)
+        xgs = {}
 
-        def x_stage(sgi):
-            xg = xgp.tile([P, 8, 4, 32, 4], BF16, align_bytes=64)
-            for b in range(4):
-                V.tensor_copy(
-                    out=xg[:, :, b, :, :],
-                    in_=xr[:, b, 8 * sgi : 8 * sgi + 8, :].rearrange("q o (t c) -> q o c t", t=4),
-                )
-            cols = slice(1024 * sgi, 1024 * sgi + 1024)
-            V.quantize_mx(
-                out=xc[:, cols].bitcast(FP8X4), scales=xs[:, cols], in_=xg[:].rearrange("q o b c t -> q (o b c t)")
+        def x_copy(grp, b):
+            if b == 0:
+                xg_new = xgp.tile([P, 8, 4, 32, 4], BF16, align_bytes=64, name="xg")
+                xgs[grp] = xg_new
+            V.tensor_copy(
+                out=xgs[grp][:, :, b, :, :],
+                in_=xr[:, b, 8 * grp : 8 * grp + 8, :].rearrange("q o (t c) -> q o c t", t=4),
             )
 
-        wg = [const.tile([P, 8192], BF16, align_bytes=64, name="wg%d" % gh) for gh in range(2)]
-        live = {}
+        def x_quant(grp):
+            cols = slice(1024 * grp, 1024 * grp + 1024)
+            V.quantize_mx(
+                out=xc[:, cols].bitcast(FP8X4), scales=xs[:, cols], in_=xgs[grp][:].rearrange("q o b c t -> q (o b c t)")
+            )
 
-        def stage_a(qq):
-            sgi, a = divmod(qq, 4)
-            ssum = sp.tile([P, 16], F32)
-            gs = []
-            for dq in range(4):
-                d = 4 * a + dq
-                cols = slice(512 * sgi, 512 * sgi + 512)
-                z = zp.tile([P, 512], F32)
-                V.scalar_tensor_tensor(
-                    out=z[:], in0=ta[:, cols], scalar=dm2[:, d : d + 1], in1=ra[:, cols], op0=ALU.mult, op1=ALU.add
+        wg = [const.tile([P, 16384], BF16, align_bytes=64, name="wg%d" % par) for par in range(2)]
+        ys = {}
+        zs = {}
+        gs = {}
+        ws = {}
+        tbs = {}
+        accs = {}
+
+        def split(j):
+            grp, r = divmod(j, 8)
+            a, l = divmod(r, 2)
+            return grp, a, l
+
+        def stage_y(j):
+            grp, a, l = split(j)
+            tq = tabs[grp][0]
+            lst = []
+            for hh in range(2):
+                d = 4 * a + 2 * hh + l
+                y = yp.tile([P, 4, P], F32)
+                V.tensor_scalar(
+                    out=y[:], in0=tq[:].rearrange("q t n p -> q t (n p)"), scalar1=dm2[:, d : d + 1], scalar2=None,
+                    op0=ALU.mult,
                 )
-                g = gp.tile([P, 2, 2, 256], F32)
-                for gh in range(2):
-                    for s in range(2):
-                        c = dq * 4 + gh * 2 + s
-                        S.activation(
-                            out=g[:, gh, s, :],
-                            in_=z[:, 256 * gh : 256 * gh + 256],
-                            func=ACTF.Exp,
-                            bias=bias[:, s, d : d + 1],
-                            scale=nha[:, s : s + 1],
-                            accum_out=ssum[:, c : c + 1],
-                        )
-                gs.append(g)
-            live[qq] = (ssum, gs)
+                lst.append(y)
+            ys[j] = lst
 
-        def stage_b(qq):
-            ssum, gs = live[qq]
-            ps = pss.tile([P, 16], F32)
-            T.matmul(out=ps[:], lhsT=pair[:].rearrange("q c e -> q (c e)"), rhs=ssum[:], start=True, stop=True)
-            tot = sp.tile([P, 16], F32)
-            V.tensor_scalar(out=tot[:], in0=ps[:], scalar1=1e-20, scalar2=None, op0=ALU.add)
-            inv = sp.tile([P, 16], F32)
-            V.reciprocal(out=inv[:], in_=tot[:])
-            ws = []
-            for dq in range(4):
-                w = wp.tile([P, 2, 2, 256], BF16)
-                for gh in range(2):
-                    for s in range(2):
-                        c = dq * 4 + gh * 2 + s
-                        V.tensor_scalar(
-                            out=w[:, gh, s, :], in0=gs[dq][:, gh, s, :], scalar1=inv[:, c : c + 1], scalar2=None,
-                            op0=ALU.mult,
-                        )
-                ws.append(w)
-            banks = {}
-            for gh in range(2):
-                for dlo in range(2):
-                    tp = ptp.tile([P, 2, 2, 2, P], BF16, tag="tp")
-                    for s in range(2):
-                        for h in range(2):
-                            for u in range(2):
-                                T.transpose(
-                                    out=tp[:, s, h, u, :],
-                                    in_=ws[2 * h + dlo][:, gh, s, P * u : P * u + P],
-                                    identity=identb[:],
-                                )
-                    banks[(gh, dlo)] = tp
-            live[qq] = banks
-
-        def stage_c(qq):
-            a = qq % 4
-            banks = live[qq]
-            for gh in range(2):
-                wv = wg[gh][:].rearrange("q (n i p a r e) -> q n i p a r e", n=4, i=4, p=16, a=4, r=4, e=2)
-                for dlo in range(2):
-                    tp = banks[(gh, dlo)]
-                    for s in range(2):
-                        dst = wv[:, :, 2 * dlo + s, :, a, :, :]
-                        src = tp[:, s].rearrange("q h u (n p e) -> q n p (h u) e", n=4, p=16, e=2)
-                        if (gh, dlo) in VECTOR_BANKS:
-                            V.tensor_copy(out=dst, in_=src)
-                        else:
-                            S.copy(out=dst, in_=src)
-
-        def stage_d(sgi):
-            for gh in range(2):
-                for n in range(4):
-                    o = 8 * sgi + 4 * gh + n
-                    wc = cp.tile([P, 512], U32, align_bytes=64)
-                    wsc = cp.tile([P, 512], U8, align_bytes=64)
-                    V.quantize_mx(out=wc[:].bitcast(FP8X4), scales=wsc[:], in_=wg[gh][:, 2048 * n : 2048 * n + 2048])
-                    acc = pacc.tile([P, 512], F32)
-                    for i in range(4):
-                        mc = slice(P * i, P * i + P)
-                        oc = slice(P * o, P * o + P)
-                        T.matmul_mx(
-                            out=acc[:, mc],
-                            lhsT=wc[:, mc].bitcast(FP8X4),
-                            lhsT_scale=wsc[:, mc],
-                            rhs=xc[:, oc].bitcast(FP8X4),
-                            rhs_scale=xs[:, oc],
-                            start=True,
-                            stop=True,
-                        )
-                    osb = op.tile([P, 4, 4, 32], F32)
-                    S.copy(out=osb[:], in_=acc[:].rearrange("q (i b c) -> q b i c", i=4, b=4))
-                    nc.sync.dma_start(
-                        out=out[:, o].rearrange("b v p (h l) s c -> (v p h) b (l s c)", l=2),
-                        in_=osb[:].rearrange("q b i c -> q b (i c)"),
+        def stage_z(j):
+            grp, a, l = split(j)
+            rq = tabs[grp][1]
+            lst = []
+            for hh in range(2):
+                zb = pz.tile([P, 4, P], F32)
+                for t in range(4):
+                    T.matmul(
+                        out=zb[:, t, :], lhsT=rq[:, t].rearrange("q n p -> q (n p)"), rhs=ident[:], is_transpose=True,
+                        start=True, stop=False,
                     )
+                    T.matmul(
+                        out=zb[:, t, :], lhsT=ys[j][hh][:, t, :], rhs=ident[:], is_transpose=True, start=False, stop=True
+                    )
+                lst.append(zb)
+            zs[j] = lst
+
+        def stage_e(j):
+            grp, a, l = split(j)
+            ssum = sp.tile([P, 4], F32)
+            lst = []
+            for hh in range(2):
+                d = 4 * a + 2 * hh + l
+                for s in range(2):
+                    g = gp.tile([P, 512], F32)
+                    S.activation(
+                        out=g[:].rearrange("m (u q e) -> m u q e", u=2, e=2),
+                        in_=zs[j][hh][:].rearrange("m (u e) q -> m u q e", e=2),
+                        func=ACTF.Exp,
+                        bias=bias[:, s, d : d + 1],
+                        scale=nha[:, s : s + 1],
+                        accum_out=ssum[:, 2 * hh + s : 2 * hh + s + 1],
+                    )
+                    lst.append(g)
+            gs[j] = (ssum, lst)
+
+        def stage_n(j):
+            ssum, lst = gs[j]
+            tot = sp.tile([P, 4], F32)
+            V.tensor_scalar(out=tot[:], in0=ssum[:], scalar1=1e-20, scalar2=None, op0=ALU.add)
+            inv = sp.tile([P, 4], F32)
+            V.reciprocal(out=inv[:], in_=tot[:])
+            wl = []
+            for c in range(4):
+                w = wp.tile([P, 512], BF16)
+                V.tensor_scalar(out=w[:], in0=lst[c][:], scalar1=inv[:, c : c + 1], scalar2=None, op0=ALU.mult)
+                wl.append(w)
+            ws[j] = wl
+
+        def stage_w(j):
+            lst = []
+            for s in range(2):
+                tb = ptp.tile([P, 2, 2, P], F32, tag="tp")
+                for hh in range(2):
+                    words = ws[j][2 * hh + s][:].bitcast(F32)
+                    for u in range(2):
+                        T.transpose(out=tb[:, hh, u, :], in_=words[:, P * u : P * u + P], identity=ident[:])
+                lst.append(tb)
+            tbs[j] = lst
+
+        def stage_c(j):
+            grp, a, l = split(j)
+            wv = wg[grp % 2][:].bitcast(F32).rearrange("q (n i p k) -> q n i p k", n=8, i=4, p=16, k=16)
+            for s in range(2):
+                S.copy(
+                    out=wv[:, :, 2 * l + s, :, 4 * a : 4 * a + 4],
+                    in_=tbs[j][s][:].rearrange("q h u (n p) -> q n p (h u)", n=8),
+                )
+
+        def node_q(grp, n):
+            o = 8 * grp + n
+            wc = cp.tile([P, 512], U32, align_bytes=64)
+            wsc = cp.tile([P, 512], U8, align_bytes=64)
+            V.quantize_mx(out=wc[:].bitcast(FP8X4), scales=wsc[:], in_=wg[grp % 2][:, 2048 * n : 2048 * n + 2048])
+            acc = pacc.tile([P, 512], F32)
+            for i in range(4):
+                mc = slice(P * i, P * i + P)
+                oc = slice(P * o, P * o + P)
+                T.matmul_mx(
+                    out=acc[:, mc],
+                    lhsT=wc[:, mc].bitcast(FP8X4),
+                    lhsT_scale=wsc[:, mc],
+                    rhs=xc[:, oc].bitcast(FP8X4),
+                    rhs_scale=xs[:, oc],
+                    start=True,
+                    stop=True,
+                )
+            accs[o] = acc
+
+        def node_o(grp, n, on_scalar):
+            o = 8 * grp + n
+            osb = op.tile([P, 4, 4, 32], F32)
+            src = accs[o][:].rearrange("q (i b c) -> q b i c", i=4, b=4)
+            if on_scalar:
+                S.copy(out=osb[:], in_=src)
+            else:
+                V.tensor_copy(out=osb[:], in_=src)
+            nc.sync.dma_start(
+                out=out[:, o].rearrange("b v p (h l) s c -> (v p h) b (l s c)", l=2),
+                in_=osb[:].rearrange("q b i c -> q b (i c)"),
+            )
 
         tables(0)
-        for step in range(18):
-            if step < 16:
-                if step % 4 == 1 and step // 4 < 3:
-                    tables(step // 4 + 1)
-                if step % 4 == 2:
-                    x_stage(step // 4)
-                stage_a(step)
-            if step >= 2:
-                stage_c(step - 2)
-                if (step - 2) % 4 == 3:
-                    stage_d((step - 2) // 4)
-            if 1 <= step <= 16:
-                stage_b(step - 1)
+        stage_y(0)
+        stage_z(0)
+        stage_y(1)
+        for j in range(N_PAIRS + 11):
+            if j + 1 < N_PAIRS:
+                stage_z(j + 1)
+            if j < N_PAIRS:
+                stage_e(j)
+            if 1 <= j <= N_PAIRS:
+                stage_n(j - 1)
+                stage_w(j - 1)
+                stage_c(j - 1)
+            if j >= 10:
+                grp, n = divmod(j - 10, 8)
+                if grp < 4:
+                    node_o(grp, n, j > N_PAIRS)
+            if j + 2 < N_PAIRS:
+                if (j + 2) % 8 == 0:
+                    tables((j + 2) // 8)
+                stage_y(j + 2)
+            if j >= 9:
+                grp, n = divmod(j - 9, 8)
+                if grp < 4:
+                    node_q(grp, n)
+            if j < N_PAIRS and 4 <= j % 8:
+                x_copy(j // 8, j % 8 - 4)
+            if 8 <= j <= N_PAIRS and j % 8 == 0:
+                x_quant(j // 8 - 1)

@@ -139,10 +139,10 @@ def tile_polnormal_nolayer_kernel(tc, x, coords_x, coords_y, phis, dists_param, 
             V.tensor_tensor(out=tx[:], in0=cq[:, 0, :, nodes].unsqueeze(3).to_broadcast(shape4), in1=trig(1), op=ALU.mult)
             ty = tmp.tile(shape4, F32)
             V.tensor_tensor(out=ty[:], in0=cq[:, 1, :, nodes].unsqueeze(3).to_broadcast(shape4), in1=trig(0), op=ALU.mult)
-            tq = tqp.tile(shape4, F32)
-            V.tensor_tensor(out=tq[:], in0=tx[:], in1=ty[:], op=ALU.add)
             rq = tqp.tile(shape4, F32)
             V.tensor_copy(out=rq[:], in_=r2q[:, :, nodes].unsqueeze(3).to_broadcast(shape4))
+            tq = tqp.tile(shape4, F32)
+            V.tensor_tensor(out=tq[:], in0=tx[:], in1=ty[:], op=ALU.add)
             tabs[grp] = (tq, rq)
 
         xc = const.tile([P, 4096], U32, align_bytes=64)
@@ -171,25 +171,24 @@ def tile_polnormal_nolayer_kernel(tc, x, coords_x, coords_y, phis, dists_param, 
         ws = {}
         tbs = {}
         accs = {}
+        tots = {}
+        invs = {}
 
         def split(j):
             grp, r = divmod(j, 8)
             a, l = divmod(r, 2)
             return grp, a, l
 
-        def stage_y(j):
+        def stage_y(j, hh):
             grp, a, l = split(j)
             tq = tabs[grp][0]
-            lst = []
-            for hh in range(2):
-                d = 4 * a + 2 * hh + l
-                y = yp.tile([P, 4, P], F32)
-                V.tensor_scalar(
-                    out=y[:], in0=tq[:].rearrange("q t n p -> q t (n p)"), scalar1=dm2[:, d : d + 1], scalar2=None,
-                    op0=ALU.mult,
-                )
-                lst.append(y)
-            ys[j] = lst
+            d = 4 * a + 2 * hh + l
+            y = yp.tile([P, 4, P], F32)
+            V.tensor_scalar(
+                out=y[:], in0=tq[:].rearrange("q t n p -> q t (n p)"), scalar1=dm2[:, d : d + 1], scalar2=None,
+                op0=ALU.mult,
+            )
+            ys[(j, hh)] = y
 
         def stage_z(j):
             grp, a, l = split(j)
@@ -203,7 +202,7 @@ def tile_polnormal_nolayer_kernel(tc, x, coords_x, coords_y, phis, dists_param, 
                         start=True, stop=False,
                     )
                     T.matmul(
-                        out=zb[:, t, :], lhsT=ys[j][hh][:, t, :], rhs=ident[:], is_transpose=True, start=False, stop=True
+                        out=zb[:, t, :], lhsT=ys[(j, hh)][:, t, :], rhs=ident[:], is_transpose=True, start=False, stop=True
                     )
                 lst.append(zb)
             zs[j] = lst
@@ -227,16 +226,22 @@ def tile_polnormal_nolayer_kernel(tc, x, coords_x, coords_y, phis, dists_param, 
                     lst.append(g)
             gs[j] = (ssum, lst)
 
-        def stage_n(j):
-            ssum, lst = gs[j]
+        def stage_tot(j):
             tot = sp.tile([P, 4], F32)
-            V.tensor_scalar(out=tot[:], in0=ssum[:], scalar1=1e-20, scalar2=None, op0=ALU.add)
+            V.tensor_scalar(out=tot[:], in0=gs[j][0][:], scalar1=1e-20, scalar2=None, op0=ALU.add)
+            tots[j] = tot
+
+        def stage_inv(j):
             inv = sp.tile([P, 4], F32)
-            V.reciprocal(out=inv[:], in_=tot[:])
+            V.reciprocal(out=inv[:], in_=tots[j][:])
+            invs[j] = inv
+
+        def stage_n(j):
+            lst = gs[j][1]
             wl = []
             for c in range(4):
                 w = wp.tile([P, 512], BF16)
-                V.tensor_scalar(out=w[:], in0=lst[c][:], scalar1=inv[:, c : c + 1], scalar2=None, op0=ALU.mult)
+                V.tensor_scalar(out=w[:], in0=lst[c][:], scalar1=invs[j][:, c : c + 1], scalar2=None, op0=ALU.mult)
                 wl.append(w)
             ws[j] = wl
 
@@ -294,26 +299,44 @@ def tile_polnormal_nolayer_kernel(tc, x, coords_x, coords_y, phis, dists_param, 
             )
 
         tables(0)
-        stage_y(0)
+        stage_y(0, 0)
+        stage_y(0, 1)
         stage_z(0)
-        stage_y(1)
+        stage_y(1, 0)
+        stage_y(1, 1)
         for j in range(N_PAIRS + 11):
             if j + 1 < N_PAIRS:
                 stage_z(j + 1)
             if j < N_PAIRS:
                 stage_e(j)
+            fill = []
+            if j >= 10 and j - 10 < 32 and j <= N_PAIRS:
+                fill.append(("o", (j - 10) // 8, (j - 10) % 8))
+            if j + 2 < N_PAIRS:
+                fill.append(("y", j + 2, 0))
+                fill.append(("y", j + 2, 1))
+
+            def take():
+                if fill:
+                    kind, a0, a1 = fill.pop(0)
+                    if kind == "o":
+                        node_o(a0, a1, False)
+                    else:
+                        stage_y(a0, a1)
+
             if 1 <= j <= N_PAIRS:
+                stage_tot(j - 1)
+                take()
+                stage_inv(j - 1)
+                take()
                 stage_n(j - 1)
                 stage_w(j - 1)
                 stage_c(j - 1)
-            if j >= 10:
-                grp, n = divmod(j - 10, 8)
-                if grp < 4:
-                    node_o(grp, n, j > N_PAIRS)
-            if j + 2 < N_PAIRS:
-                if (j + 2) % 8 == 0:
-                    tables((j + 2) // 8)
-                stage_y(j + 2)
+            take()
+            take()
+            take()
+            if j > N_PAIRS and j - 10 < 32:
+                node_o((j - 10) // 8, (j - 10) % 8, True)
             if j >= 9:
                 grp, n = divmod(j - 9, 8)
                 if grp < 4:
@@ -322,3 +345,5 @@ def tile_polnormal_nolayer_kernel(tc, x, coords_x, coords_y, phis, dists_param, 
                 x_copy(j // 8, j % 8 - 4)
             if 8 <= j <= N_PAIRS and j % 8 == 0:
                 x_quant(j // 8 - 1)
+            if (j + 3) % 8 == 0 and j + 3 < N_PAIRS:
+                tables((j + 3) // 8)

@@ -18,8 +18,6 @@ ACTF = mybir.ActivationFunctionType
 P = 128
 FLOPS = 2 * 32 * 512 * 512 * 128
 
-TWO_PI_HI = 6.28125
-TWO_PI_LO = 2.0 * math.pi - 6.28125
 PI_F32 = 3.1415927410125732
 
 N_PAIRS = 32
@@ -46,16 +44,17 @@ def tile_polnormal_nolayer_kernel(tc, x, coords_x, coords_y, phis, dists_param, 
         pacc = ctx.enter_context(tc.psum_pool(name="pacc", bufs=2))
         ctx.enter_context(nc.allow_non_contiguous_dma(reason="rows of 256 and 512 bytes"))
 
+        pv = const.tile([P, 64], BF16)
+        V.memset(pv[:].bitcast(I32), 0)
         cn = const.tile([P, 512], BF16)
-        V.memset(cn[:].bitcast(I32), 0)
         nc.sync.dma_start(out=cn[0:32, :], in_=coords_x.rearrange("a o i j -> (a o) (i j)"))
         nc.sync.dma_start(out=cn[32:64, :], in_=coords_y.rearrange("a o i j -> (a o) (i j)"))
-        phr = const.tile([P, 16], BF16)
-        nc.sync.dma_start(out=phr[:], in_=phis.partition_broadcast(P))
-        dpr = const.tile([P, 16], BF16)
-        nc.sync.dma_start(out=dpr[:], in_=dists_param.partition_broadcast(P))
-        spr = const.tile([P, 2], BF16)
-        nc.sync.dma_start(out=spr[:], in_=sigma_param.partition_broadcast(P))
+        nc.sync.dma_start(out=pv[0:1, 0:16], in_=phis.unsqueeze(0))
+        nc.sync.dma_start(out=pv[0:1, 16:32], in_=dists_param.unsqueeze(0))
+        nc.sync.dma_start(out=pv[0:1, 32:34], in_=sigma_param.unsqueeze(0))
+        V.memset(cn[64:128, :].bitcast(I32), 0)
+        ones = const.tile([P, P], BF16)
+        V.memset(ones[:], 1.0)
         xr = const.tile([P, 4, 32, 128], BF16)
         for b in range(4):
             nc.sync.dma_start(
@@ -67,64 +66,65 @@ def tile_polnormal_nolayer_kernel(tc, x, coords_x, coords_y, phis, dists_param, 
         identb = const.tile([P, P], BF16)
         make_identity(nc, identb[:])
 
+        warm = const.tile([P, 1], F32)
+        V.memset(warm[:], 0.0)
+        S.activation(out=warm[:], in_=warm[:], func=ACTF.Silu)
+        pp = ptp.tile([P, 64], F32, tag="tp")
+        T.matmul(out=pp[:], lhsT=ones[:], rhs=pv[:], start=True, stop=True)
+        pvs = const.tile([P, 64], F32)
+        V.tensor_copy(out=pvs[:], in_=pp[:])
+        phr = pvs[:, 0:16]
+        dpr = pvs[:, 16:32]
+        spr = pvs[:, 32:34]
         thd = const.tile([P, 16], F32)
-        S.activation(out=thd[:], in_=dpr[:], func=ACTF.Tanh, scale=0.5)
+        S.activation(out=thd[:], in_=dpr, func=ACTF.Tanh, scale=0.5)
         ths = const.tile([P, 2], F32)
-        S.activation(out=ths[:], in_=spr[:], func=ACTF.Tanh, scale=0.5)
-        dm2 = const.tile([P, 16], F32)
-        V.tensor_scalar(out=dm2[:], in0=thd[:], scalar1=1.0, scalar2=-2.0, op0=ALU.add, op1=ALU.mult)
-        dd = const.tile([P, 16], F32)
-        V.tensor_scalar(out=dd[:], in0=thd[:], scalar1=1.0, scalar2=None, op0=ALU.add)
-        dsq = const.tile([P, 16], F32)
-        V.tensor_tensor(out=dsq[:], in0=dd[:], in1=dd[:], op=ALU.mult)
-        sg = const.tile([P, 2], F32)
-        V.tensor_scalar(out=sg[:], in0=ths[:], scalar1=1.0, scalar2=1e-10, op0=ALU.add, op1=ALU.max)
-        sg2 = const.tile([P, 2], F32)
-        V.tensor_tensor(out=sg2[:], in0=sg[:], in1=sg[:], op=ALU.mult)
-        rsg = const.tile([P, 2], F32)
-        V.reciprocal(out=rsg[:], in_=sg2[:])
-        nha = const.tile([P, 2], F32)
-        V.tensor_scalar(out=nha[:], in0=rsg[:], scalar1=-0.5, scalar2=None, op0=ALU.mult)
-        bias = const.tile([P, 2, 16], F32)
-        for s in range(2):
-            V.tensor_scalar(out=bias[:, s, :], in0=dsq[:], scalar1=nha[:, s : s + 1], scalar2=None, op0=ALU.mult)
+        S.activation(out=ths[:], in_=spr, func=ACTF.Tanh, scale=0.5)
 
-        phf = const.tile([P, 16], F32)
-        V.tensor_copy(out=phf[:], in_=phr[:])
         qi = const.tile([P, 16], I32)
-        V.tensor_scalar(out=qi[:], in0=phf[:], scalar1=1.0 / (2.0 * math.pi), scalar2=None, op0=ALU.mult)
-        qf = const.tile([P, 16], F32)
-        V.tensor_copy(out=qf[:], in_=qi[:])
-        p1 = const.tile([P, 16], F32)
-        V.scalar_tensor_tensor(out=p1[:], in0=qf[:], scalar=-TWO_PI_HI, in1=phf[:], op0=ALU.mult, op1=ALU.add)
-        p2 = const.tile([P, 16], F32)
-        V.scalar_tensor_tensor(out=p2[:], in0=qf[:], scalar=-TWO_PI_LO, in1=p1[:], op0=ALU.mult, op1=ALU.add)
-        over = const.tile([P, 16], F32)
-        V.tensor_scalar(out=over[:], in0=p2[:], scalar1=PI_F32, scalar2=-1.0, op0=ALU.is_gt, op1=ALU.mult)
-        turn = const.tile([P, 16], F32)
-        V.scalar_tensor_tensor(out=turn[:], in0=p2[:], scalar=-PI_F32, in1=over[:], op0=ALU.is_lt, op1=ALU.add)
-        p3 = const.tile([P, 16], F32)
-        V.scalar_tensor_tensor(out=p3[:], in0=turn[:], scalar=TWO_PI_HI, in1=p2[:], op0=ALU.mult, op1=ALU.add)
-        ang = const.tile([P, 2, 16], F32)
-        V.scalar_tensor_tensor(out=ang[:, 0, :], in0=turn[:], scalar=TWO_PI_LO, in1=p3[:], op0=ALU.mult, op1=ALU.add)
-        aab = const.tile([P, 16], F32)
-        V.scalar_tensor_tensor(out=aab[:], in0=ang[:, 0, :], scalar=-1.0, in1=ang[:, 0, :], op0=ALU.mult, op1=ALU.max)
-        V.tensor_scalar(out=ang[:, 1, :], in0=aab[:], scalar1=-1.0, scalar2=0.5 * math.pi, op0=ALU.mult, op1=ALU.add)
-        cs = const.tile([P, 2, 16], F32)
-        S.activation(out=cs[:], in_=ang[:], func=ACTF.Sin)
-
+        V.tensor_scalar(out=qi[:], in0=phr, scalar1=1.0 / (2.0 * math.pi), scalar2=None, op0=ALU.mult)
         cn2 = const.tile([P, 4, P], BF16)
         V.tensor_copy(out=cn2[:], in_=cn[:].rearrange("r (q t) -> r t q", t=4))
         pc = ptp.tile([P, 4, P], BF16, tag="tp")
         for t in range(4):
             T.transpose(out=pc[:, t, :], in_=cn2[:, t, :], identity=identb[:])
+        qf = const.tile([P, 16], F32)
+        V.tensor_copy(out=qf[:], in_=qi[:])
+        dm2 = const.tile([P, 16], F32)
+        V.tensor_scalar(out=dm2[:], in0=thd[:], scalar1=1.0, scalar2=-2.0, op0=ALU.add, op1=ALU.mult)
+        p2 = const.tile([P, 16], F32)
+        V.scalar_tensor_tensor(out=p2[:], in0=qf[:], scalar=-2.0 * math.pi, in1=phr, op0=ALU.mult, op1=ALU.add)
+        dd = const.tile([P, 16], F32)
+        V.tensor_scalar(out=dd[:], in0=thd[:], scalar1=1.0, scalar2=None, op0=ALU.add)
+        over = const.tile([P, 16], F32)
+        V.tensor_scalar(out=over[:], in0=p2[:], scalar1=PI_F32, scalar2=-1.0, op0=ALU.is_gt, op1=ALU.mult)
+        sg = const.tile([P, 2], F32)
+        V.tensor_scalar(out=sg[:], in0=ths[:], scalar1=1.0, scalar2=1e-10, op0=ALU.add, op1=ALU.max)
+        turn = const.tile([P, 16], F32)
+        V.scalar_tensor_tensor(out=turn[:], in0=p2[:], scalar=-PI_F32, in1=over[:], op0=ALU.is_lt, op1=ALU.add)
+        dsq = const.tile([P, 16], F32)
+        V.tensor_tensor(out=dsq[:], in0=dd[:], in1=dd[:], op=ALU.mult)
+        ang = const.tile([P, 16], F32)
+        V.scalar_tensor_tensor(out=ang[:], in0=turn[:], scalar=2.0 * math.pi, in1=p2[:], op0=ALU.mult, op1=ALU.add)
+        sgm = const.tile([P, 2], F32)
+        V.scalar_tensor_tensor(out=sgm[:], in0=sg[:], scalar=-2.0, in1=sg[:], op0=ALU.mult, op1=ALU.mult)
+        aab = const.tile([P, 16], F32)
+        V.scalar_tensor_tensor(out=aab[:], in0=ang[:], scalar=-1.0, in1=ang[:], op0=ALU.mult, op1=ALU.max)
+        cs = const.tile([P, 2, 16], F32)
+        S.activation(out=cs[:, 0, :], in_=ang[:], func=ACTF.Sin)
+        S.activation(out=cs[:, 1, :], in_=aab[:], func=ACTF.Sin, scale=-1.0, bias=0.5 * math.pi)
         cq = const.tile([P, 2, 4, 32], F32)
         V.tensor_copy(out=cq[:], in_=pc[:, :, 0:64].rearrange("q t (a o) -> q a t o", a=2))
+        nha = const.tile([P, 2], F32)
+        V.reciprocal(out=nha[:], in_=sgm[:])
         sq = const.tile([P, 2, P], F32)
         cqf = cq[:].rearrange("q a t o -> q a (t o)")
         V.tensor_tensor(out=sq[:], in0=cqf, in1=cqf, op=ALU.mult)
+        bias = const.tile([P, 2, 16], F32)
+        V.tensor_scalar(out=bias[:, 0, :], in0=dsq[:], scalar1=nha[:, 0:1], scalar2=None, op0=ALU.mult)
         r2q = const.tile([P, 4, 32], F32)
         V.tensor_tensor(out=r2q[:].rearrange("q t o -> q (t o)"), in0=sq[:, 0, :], in1=sq[:, 1, :], op=ALU.add)
+        V.tensor_scalar(out=bias[:, 1, :], in0=dsq[:], scalar1=nha[:, 1:2], scalar2=None, op0=ALU.mult)
 
         shape4 = [P, 4, 8, 16]
         tabs = {}

@@ -154,8 +154,8 @@ def tile_polnormal_nolayer_kernel(tc, x, coords_x, coords_y, phis, dists_param, 
                 xg_new = xgp.tile([P, 8, 4, 32, 4], BF16, align_bytes=64, name="xg")
                 xgs[grp] = xg_new
             V.tensor_copy(
-                out=xgs[grp][:, :, b, :, :],
-                in_=xr[:, b, 8 * grp : 8 * grp + 8, :].rearrange("q o (t c) -> q o c t", t=4),
+                out=xgs[grp][:, :, b, :, :].rearrange("q o (k i) t -> q o k t i", i=4),
+                in_=xr[:, b, 8 * grp : 8 * grp + 8, :].rearrange("q o (t k i) -> q o k t i", t=4, i=4),
             )
 
         def x_quant(grp):

@@ -20,7 +20,9 @@ FLOPS = 2 * 32 * 512 * 512 * 128
 
 PI_F32 = 3.1415927410125732
 
-N_PAIRS = 32
+NODES = 32
+GROUPS = (2, 2, 4, 8, 8, 8)
+STARTS = (0, 2, 4, 8, 16, 24)
 
 
 def tile_polnormal_nolayer_kernel(tc, x, coords_x, coords_y, phis, dists_param, sigma_param, out):
@@ -32,7 +34,8 @@ def tile_polnormal_nolayer_kernel(tc, x, coords_x, coords_y, phis, dists_param, 
         const = ctx.enter_context(tc.tile_pool(name="const", bufs=1))
         tmp = ctx.enter_context(tc.tile_pool(name="tmp", bufs=2))
         tqp = ctx.enter_context(tc.tile_pool(name="tqp", bufs=2))
-        yp = ctx.enter_context(tc.tile_pool(name="yp", bufs=4))
+        yp = ctx.enter_context(tc.tile_pool(name="yp", bufs=3))
+        wgp = ctx.enter_context(tc.tile_pool(name="wgp", bufs=3))
         gp = ctx.enter_context(tc.tile_pool(name="gp", bufs=10))
         wp = ctx.enter_context(tc.tile_pool(name="wp", bufs=8))
         sp = ctx.enter_context(tc.tile_pool(name="sp", bufs=3))
@@ -47,231 +50,223 @@ def tile_polnormal_nolayer_kernel(tc, x, coords_x, coords_y, phis, dists_param, 
         pv = const.tile([P, 64], BF16)
         V.memset(pv[:].bitcast(I32), 0)
         cn = const.tile([P, 512], BF16)
-        nc.sync.dma_start(out=cn[0:32, :], in_=coords_x.rearrange("a o i j -> (a o) (i j)"))
-        nc.sync.dma_start(out=cn[32:64, :], in_=coords_y.rearrange("a o i j -> (a o) (i j)"))
         nc.sync.dma_start(out=pv[0:1, 0:16], in_=phis.unsqueeze(0))
         nc.sync.dma_start(out=pv[0:1, 16:32], in_=dists_param.unsqueeze(0))
         nc.sync.dma_start(out=pv[0:1, 32:34], in_=sigma_param.unsqueeze(0))
+        nc.sync.dma_start(out=cn[0:32, :], in_=coords_x.rearrange("a o i j -> (a o) (i j)"))
+        nc.sync.dma_start(out=cn[32:64, :], in_=coords_y.rearrange("a o i j -> (a o) (i j)"))
         V.memset(cn[64:128, :].bitcast(I32), 0)
         ones = const.tile([P, P], BF16)
         V.memset(ones[:], 1.0)
         xr = const.tile([P, 4, 32, 128], BF16)
-        for b in range(4):
-            nc.sync.dma_start(
-                out=xr[:, b], in_=x[b].rearrange("(o q t) a v c -> q o (t a v c)", o=32, q=P, t=4)
-            )
+        for grp in range(len(GROUPS)):
+            nodes = slice(STARTS[grp], STARTS[grp] + GROUPS[grp])
+            for b in range(4):
+                nc.sync.dma_start(
+                    out=xr[:, b, nodes, :],
+                    in_=x[b].rearrange("(o q t) a v c -> q o (t a v c)", o=32, q=P, t=4)[:, nodes, :],
+                )
 
         ident = const.tile([P, P], F32)
         make_identity(nc, ident[:])
         identb = const.tile([P, P], BF16)
         make_identity(nc, identb[:])
+        identp = const.tile([P, P], F32)
+        V.tensor_copy(out=identp[:].rearrange("k (p h) -> k p h", h=8), in_=ident[:].rearrange("k (h p) -> k p h", p=16))
 
         warm = const.tile([P, 1], F32)
         V.memset(warm[:], 0.0)
         S.activation(out=warm[:], in_=warm[:], func=ACTF.Silu)
         pp = ptp.tile([P, 64], F32, tag="tp")
         T.matmul(out=pp[:], lhsT=ones[:], rhs=pv[:], start=True, stop=True)
-        pvs = const.tile([P, 64], F32)
-        V.tensor_copy(out=pvs[:], in_=pp[:])
-        phr = pvs[:, 0:16]
-        dpr = pvs[:, 16:32]
-        spr = pvs[:, 32:34]
-        thd = const.tile([P, 16], F32)
-        S.activation(out=thd[:], in_=dpr, func=ACTF.Tanh, scale=0.5)
-        ths = const.tile([P, 2], F32)
-        S.activation(out=ths[:], in_=spr, func=ACTF.Tanh, scale=0.5)
-
-        qi = const.tile([P, 16], I32)
-        V.tensor_scalar(out=qi[:], in0=phr, scalar1=1.0 / (2.0 * math.pi), scalar2=None, op0=ALU.mult)
-        cn2 = const.tile([P, 4, P], BF16)
-        V.tensor_copy(out=cn2[:], in_=cn[:].rearrange("r (q t) -> r t q", t=4))
+        ph = const.tile([P, 2, 16], F32)
+        V.tensor_scalar(out=ph[:, 1, :], in0=pp[:, 0:16], scalar1=0.5 * math.pi, scalar2=None, op0=ALU.add)
+        V.tensor_copy(out=ph[:, 0, :], in_=pp[:, 0:16])
+        th = const.tile([P, 18], F32)
+        S.activation(out=th[:], in_=pp[:, 16:34], func=ACTF.Tanh, scale=0.5)
+        qi = const.tile([P, 2, 16], I32)
+        V.tensor_scalar(out=qi[:], in0=ph[:], scalar1=1.0 / (2.0 * math.pi), scalar2=None, op0=ALU.mult)
         pc = ptp.tile([P, 4, P], BF16, tag="tp")
+        cells = cn[:].rearrange("r (q t) -> r t q", t=4)
         for t in range(4):
-            T.transpose(out=pc[:, t, :], in_=cn2[:, t, :], identity=identb[:])
-        qf = const.tile([P, 16], F32)
-        V.tensor_copy(out=qf[:], in_=qi[:])
+            T.transpose(out=pc[:, t, :], in_=cells[:, t, :], identity=identb[:])
+        pcv = pc[:, :, 0:64].rearrange("q t (a o) -> q a t o", a=2)
+        p2 = const.tile([P, 2, 16], F32)
+        V.scalar_tensor_tensor(out=p2[:], in0=qi[:], scalar=-2.0 * math.pi, in1=ph[:], op0=ALU.mult, op1=ALU.add)
+        cq = const.tile([P, 2, 4, 32], F32)
+        S.copy(out=cq[:], in_=pcv)
+        ang = const.tile([P, 2, 16], F32)
+        V.tensor_scalar(out=ang[:], in0=p2[:], scalar1=-PI_F32, scalar2=PI_F32, op0=ALU.max, op1=ALU.min)
         dm2 = const.tile([P, 16], F32)
-        V.tensor_scalar(out=dm2[:], in0=thd[:], scalar1=1.0, scalar2=-2.0, op0=ALU.add, op1=ALU.mult)
-        p2 = const.tile([P, 16], F32)
-        V.scalar_tensor_tensor(out=p2[:], in0=qf[:], scalar=-2.0 * math.pi, in1=phr, op0=ALU.mult, op1=ALU.add)
+        V.tensor_scalar(out=dm2[:], in0=th[:, 0:16], scalar1=1.0, scalar2=-2.0, op0=ALU.add, op1=ALU.mult)
+        cs = const.tile([P, 2, 16], F32)
+        S.activation(out=cs[:], in_=ang[:], func=ACTF.Sin)
         dd = const.tile([P, 16], F32)
-        V.tensor_scalar(out=dd[:], in0=thd[:], scalar1=1.0, scalar2=None, op0=ALU.add)
-        over = const.tile([P, 16], F32)
-        V.tensor_scalar(out=over[:], in0=p2[:], scalar1=PI_F32, scalar2=-1.0, op0=ALU.is_gt, op1=ALU.mult)
+        V.tensor_scalar(out=dd[:], in0=th[:, 0:16], scalar1=1.0, scalar2=None, op0=ALU.add)
+        sq = const.tile([P, 2, 4, 32], F32)
+        S.activation(out=sq[:], in_=pcv, func=ACTF.Square)
         sg = const.tile([P, 2], F32)
-        V.tensor_scalar(out=sg[:], in0=ths[:], scalar1=1.0, scalar2=1e-10, op0=ALU.add, op1=ALU.max)
-        turn = const.tile([P, 16], F32)
-        V.scalar_tensor_tensor(out=turn[:], in0=p2[:], scalar=-PI_F32, in1=over[:], op0=ALU.is_lt, op1=ALU.add)
+        V.tensor_scalar(out=sg[:], in0=th[:, 16:18], scalar1=1.0, scalar2=1e-10, op0=ALU.add, op1=ALU.max)
         dsq = const.tile([P, 16], F32)
         V.tensor_tensor(out=dsq[:], in0=dd[:], in1=dd[:], op=ALU.mult)
-        ang = const.tile([P, 16], F32)
-        V.scalar_tensor_tensor(out=ang[:], in0=turn[:], scalar=2.0 * math.pi, in1=p2[:], op0=ALU.mult, op1=ALU.add)
         sgm = const.tile([P, 2], F32)
         V.scalar_tensor_tensor(out=sgm[:], in0=sg[:], scalar=-2.0, in1=sg[:], op0=ALU.mult, op1=ALU.mult)
-        aab = const.tile([P, 16], F32)
-        V.scalar_tensor_tensor(out=aab[:], in0=ang[:], scalar=-1.0, in1=ang[:], op0=ALU.mult, op1=ALU.max)
-        cs = const.tile([P, 2, 16], F32)
-        S.activation(out=cs[:, 0, :], in_=ang[:], func=ACTF.Sin)
-        S.activation(out=cs[:, 1, :], in_=aab[:], func=ACTF.Sin, scale=-1.0, bias=0.5 * math.pi)
-        cq = const.tile([P, 2, 4, 32], F32)
-        V.tensor_copy(out=cq[:], in_=pc[:, :, 0:64].rearrange("q t (a o) -> q a t o", a=2))
         nha = const.tile([P, 2], F32)
         V.reciprocal(out=nha[:], in_=sgm[:])
-        sq = const.tile([P, 2, P], F32)
-        cqf = cq[:].rearrange("q a t o -> q a (t o)")
-        V.tensor_tensor(out=sq[:], in0=cqf, in1=cqf, op=ALU.mult)
-        bias = const.tile([P, 2, 16], F32)
-        V.tensor_scalar(out=bias[:, 0, :], in0=dsq[:], scalar1=nha[:, 0:1], scalar2=None, op0=ALU.mult)
         r2q = const.tile([P, 4, 32], F32)
-        V.tensor_tensor(out=r2q[:].rearrange("q t o -> q (t o)"), in0=sq[:, 0, :], in1=sq[:, 1, :], op=ALU.add)
-        V.tensor_scalar(out=bias[:, 1, :], in0=dsq[:], scalar1=nha[:, 1:2], scalar2=None, op0=ALU.mult)
+        V.tensor_tensor(out=r2q[:], in0=sq[:, 0], in1=sq[:, 1], op=ALU.add)
 
-        shape4 = [P, 4, 8, 16]
-        tabs = {}
+        tqs = {}
+        yts = {}
 
         def tables(grp):
-            nodes = slice(8 * grp, 8 * grp + 8)
+            size = GROUPS[grp]
+            nodes = slice(STARTS[grp], STARTS[grp] + size)
+            shape = [P, size, 4, 16]
 
             def trig(row):
-                return cs[:, row, :].unsqueeze(1).unsqueeze(1).to_broadcast(shape4)
+                return cs[:, row, :].unsqueeze(1).unsqueeze(1).to_broadcast(shape)
 
-            tx = tmp.tile(shape4, F32)
-            V.tensor_tensor(out=tx[:], in0=cq[:, 0, :, nodes].unsqueeze(3).to_broadcast(shape4), in1=trig(1), op=ALU.mult)
-            ty = tmp.tile(shape4, F32)
-            V.tensor_tensor(out=ty[:], in0=cq[:, 1, :, nodes].unsqueeze(3).to_broadcast(shape4), in1=trig(0), op=ALU.mult)
-            rq = tqp.tile(shape4, F32)
-            V.tensor_copy(out=rq[:], in_=r2q[:, :, nodes].unsqueeze(3).to_broadcast(shape4))
-            tq = tqp.tile(shape4, F32)
+            def coord(row):
+                return cq[:, row, :, nodes].rearrange("q t o -> q o t").unsqueeze(3).to_broadcast(shape)
+
+            tx = tmp.tile(shape, F32, name="tx")
+            V.tensor_tensor(out=tx[:], in0=coord(0), in1=trig(1), op=ALU.mult)
+            ty = tmp.tile(shape, F32, name="ty")
+            V.tensor_tensor(out=ty[:], in0=coord(1), in1=trig(0), op=ALU.mult)
+            tq = tqp.tile(shape, F32, name="tq")
             V.tensor_tensor(out=tq[:], in0=tx[:], in1=ty[:], op=ALU.add)
-            tabs[grp] = (tq, rq)
+            tqs[grp] = tq
+            y = yp.tile([P, size, 4, 2, 8, 16], F32, name="y")
+            yts[grp] = y
+
+        def stage_y(grp, l, h):
+            d = 2 * h + l
+            V.tensor_scalar(
+                out=yts[grp][:, :, :, l, h, :], in0=tqs[grp][:], scalar1=dm2[:, d : d + 1], scalar2=dsq[:, d : d + 1],
+                op0=ALU.mult, op1=ALU.add,
+            )
 
         xc = const.tile([P, 4096], U32, align_bytes=64)
         xs = const.tile([P, 4096], U8, align_bytes=64)
         xgs = {}
 
         def x_copy(grp, b):
+            size = GROUPS[grp]
             if b == 0:
-                xg_new = xgp.tile([P, 8, 4, 32, 4], BF16, align_bytes=64, name="xg")
+                xg_new = xgp.tile([P, size, 4, 32, 4], BF16, align_bytes=64, name="xg")
                 xgs[grp] = xg_new
             V.tensor_copy(
                 out=xgs[grp][:, :, b, :, :].rearrange("q o (k i) t -> q o k t i", i=4),
-                in_=xr[:, b, 8 * grp : 8 * grp + 8, :].rearrange("q o (t k i) -> q o k t i", t=4, i=4),
+                in_=xr[:, b, STARTS[grp] : STARTS[grp] + size, :].rearrange("q o (t k i) -> q o k t i", t=4, i=4),
             )
 
-        def x_quant(grp):
-            cols = slice(1024 * grp, 1024 * grp + 1024)
+        def x_quant(grp, first, size):
+            o = STARTS[grp] + first
+            cols = slice(128 * o, 128 * (o + size))
             V.quantize_mx(
-                out=xc[:, cols].bitcast(FP8X4), scales=xs[:, cols], in_=xgs[grp][:].rearrange("q o b c t -> q (o b c t)")
+                out=xc[:, cols].bitcast(FP8X4), scales=xs[:, cols],
+                in_=xgs[grp][:, first : first + size].rearrange("q o b c t -> q (o b c t)"),
             )
 
-        wg = [const.tile([P, 16384], BF16, align_bytes=64, name="wg%d" % par) for par in range(2)]
-        ys = {}
         zs = {}
         gs = {}
         ws = {}
         tbs = {}
+        wgs = {}
         accs = {}
         tots = {}
         invs = {}
 
-        def split(j):
-            grp, r = divmod(j, 8)
-            a, l = divmod(r, 2)
-            return grp, a, l
+        def group_of(o):
+            grp = max(g for g in range(len(GROUPS)) if STARTS[g] <= o)
+            return grp, o - STARTS[grp]
 
-        def stage_y(j, hh):
-            grp, a, l = split(j)
-            tq = tabs[grp][0]
-            d = 4 * a + 2 * hh + l
-            y = yp.tile([P, 4, P], F32)
-            V.tensor_scalar(
-                out=y[:], in0=tq[:].rearrange("q t n p -> q t (n p)"), scalar1=dm2[:, d : d + 1], scalar2=None,
-                op0=ALU.mult,
-            )
-            ys[(j, hh)] = y
-
-        def stage_z(j):
-            grp, a, l = split(j)
-            rq = tabs[grp][1]
+        def stage_z(o):
+            grp, n = group_of(o)
             lst = []
-            for hh in range(2):
+            for l in range(2):
                 zb = pz.tile([P, 4, P], F32)
                 for t in range(4):
                     T.matmul(
-                        out=zb[:, t, :], lhsT=rq[:, t].rearrange("q n p -> q (n p)"), rhs=ident[:], is_transpose=True,
+                        out=zb[:, t, :], lhsT=r2q[:, t, o : o + 1].to_broadcast([P, P]), rhs=ident[:], is_transpose=True,
                         start=True, stop=False,
                     )
                     T.matmul(
-                        out=zb[:, t, :], lhsT=ys[(j, hh)][:, t, :], rhs=ident[:], is_transpose=True, start=False, stop=True
+                        out=zb[:, t, :], lhsT=yts[grp][:, n, t, l].rearrange("q h p -> q (h p)"), rhs=ident[:],
+                        is_transpose=True, start=False, stop=True,
                     )
                 lst.append(zb)
-            zs[j] = lst
+            zs[o] = lst
 
-        def stage_e(j):
-            grp, a, l = split(j)
+        def stage_e(o):
             ssum = sp.tile([P, 4], F32)
             lst = []
-            for hh in range(2):
-                d = 4 * a + 2 * hh + l
+            for l in range(2):
                 for s in range(2):
                     g = gp.tile([P, 512], F32)
                     S.activation(
                         out=g[:].rearrange("m (u q e) -> m u q e", u=2, e=2),
-                        in_=zs[j][hh][:].rearrange("m (u e) q -> m u q e", e=2),
+                        in_=zs[o][l][:].rearrange("m (u e) q -> m u q e", e=2),
                         func=ACTF.Exp,
-                        bias=bias[:, s, d : d + 1],
                         scale=nha[:, s : s + 1],
-                        accum_out=ssum[:, 2 * hh + s : 2 * hh + s + 1],
+                        accum_out=ssum[:, 2 * l + s : 2 * l + s + 1],
                     )
                     lst.append(g)
-            gs[j] = (ssum, lst)
+            gs[o] = (ssum, lst)
 
-        def stage_tot(j):
-            tot = sp.tile([P, 4], F32)
-            V.tensor_scalar(out=tot[:], in0=gs[j][0][:], scalar1=1e-20, scalar2=None, op0=ALU.add)
-            tots[j] = tot
+        def stage_tot(o, ls):
+            ssum = gs[o][0]
+            tot = sp.tile([P, 2 * len(ls)], F32)
+            V.tensor_scalar(
+                out=tot[:], in0=ssum[:, 2 * ls[0] : 2 * ls[-1] + 2], scalar1=1e-20, scalar2=None, op0=ALU.add
+            )
+            tots[o] = tot
 
-        def stage_inv(j):
-            inv = sp.tile([P, 4], F32)
-            V.reciprocal(out=inv[:], in_=tots[j][:])
-            invs[j] = inv
+        def stage_inv(o, ls):
+            inv = sp.tile([P, 2 * len(ls)], F32)
+            V.reciprocal(out=inv[:], in_=tots[o][:])
+            for l in ls:
+                for s in range(2):
+                    c = 2 * (l - ls[0]) + s
+                    invs[(o, l, s)] = inv[:, c : c + 1]
 
-        def stage_n(j):
-            lst = gs[j][1]
-            wl = []
-            for c in range(4):
-                w = wp.tile([P, 512], BF16)
-                V.tensor_scalar(out=w[:], in0=lst[c][:], scalar1=invs[j][:, c : c + 1], scalar2=None, op0=ALU.mult)
-                wl.append(w)
-            ws[j] = wl
+        def stage_n(o, ls):
+            for l in ls:
+                for s in range(2):
+                    w = wp.tile([P, 512], BF16)
+                    V.tensor_scalar(
+                        out=w[:], in0=gs[o][1][2 * l + s][:], scalar1=invs[(o, l, s)], scalar2=None, op0=ALU.mult
+                    )
+                    ws[(o, l, s)] = w
 
-        def stage_w(j):
-            lst = []
-            for s in range(2):
+        def stage_w(o, ls):
+            for l in ls:
                 tb = ptp.tile([P, 2, 2, P], F32, tag="tp")
-                for hh in range(2):
-                    words = ws[j][2 * hh + s][:].bitcast(F32)
+                for s in range(2):
+                    words = ws[(o, l, s)][:].bitcast(F32)
                     for u in range(2):
-                        T.transpose(out=tb[:, hh, u, :], in_=words[:, P * u : P * u + P], identity=ident[:])
-                lst.append(tb)
-            tbs[j] = lst
+                        T.transpose(out=tb[:, s, u, :], in_=words[:, P * u : P * u + P], identity=identp[:])
+                tbs[(o, l)] = tb
 
-        def stage_c(j):
-            grp, a, l = split(j)
-            wv = wg[grp % 2][:].bitcast(F32).rearrange("q (n i p k) -> q n i p k", n=8, i=4, p=16, k=16)
-            for s in range(2):
-                S.copy(
-                    out=wv[:, :, 2 * l + s, :, 4 * a : 4 * a + 4],
-                    in_=tbs[j][s][:].rearrange("q h u (n p) -> q n p (h u)", n=8),
-                )
+        def stage_c(o, ls):
+            if o not in wgs:
+                wg = wgp.tile([P, 2048], BF16, align_bytes=64)
+                wgs[o] = wg
+            wv = wgs[o][:].bitcast(F32).rearrange("q (i n u) -> q i n u", i=4, u=2)
+            for l in ls:
+                S.copy(out=wv[:, 2 * l : 2 * l + 2], in_=tbs[(o, l)][:].rearrange("q s u n -> q s n u"))
 
-        def node_q(grp, n):
-            o = 8 * grp + n
+        def node_q(o, ls):
+            first, last = 2 * ls[0], 2 * ls[-1] + 2
+            cols = slice(P * first, P * last)
             wc = cp.tile([P, 512], U32, align_bytes=64)
             wsc = cp.tile([P, 512], U8, align_bytes=64)
-            V.quantize_mx(out=wc[:].bitcast(FP8X4), scales=wsc[:], in_=wg[grp % 2][:, 2048 * n : 2048 * n + 2048])
+            V.quantize_mx(
+                out=wc[:, cols].bitcast(FP8X4), scales=wsc[:, cols], in_=wgs[o][:, 512 * first : 512 * last]
+            )
             acc = pacc.tile([P, 512], F32)
-            for i in range(4):
+            for i in range(first, last):
                 mc = slice(P * i, P * i + P)
                 oc = slice(P * o, P * o + P)
                 T.matmul_mx(
@@ -283,67 +278,82 @@ def tile_polnormal_nolayer_kernel(tc, x, coords_x, coords_y, phis, dists_param, 
                     start=True,
                     stop=True,
                 )
-            accs[o] = acc
+            accs[(o, ls)] = acc
 
-        def node_o(grp, n, on_scalar):
-            o = 8 * grp + n
-            osb = op.tile([P, 4, 4, 32], F32)
-            src = accs[o][:].rearrange("q (i b c) -> q b i c", i=4, b=4)
+        def node_o(o, ls, on_scalar):
+            osb = op.tile([P, 4, 2 * len(ls), 32], F32)
+            src = accs[(o, ls)][:, 256 * ls[0] : 256 * ls[-1] + 256].rearrange("q (i b c) -> q b i c", b=4, c=32)
             if on_scalar:
                 S.copy(out=osb[:], in_=src)
             else:
                 V.tensor_copy(out=osb[:], in_=src)
-            nc.sync.dma_start(
-                out=out[:, o].rearrange("b v p (h l) s c -> (v p h) b (l s c)", l=2),
-                in_=osb[:].rearrange("q b i c -> q b (i c)"),
-            )
+            dst = out[:, o, 0].rearrange("b p (h l) s c -> (p h) b l (s c)", l=2)
+            if len(ls) == 2:
+                dst = dst.rearrange("m b l k -> m b (l k)")
+            else:
+                dst = dst[:, :, ls[0], :]
+            nc.sync.dma_start(out=dst, in_=osb[:].rearrange("q b i c -> q b (i c)"))
 
+        jobs = {}
+
+        def job(step, fn, *args):
+            jobs.setdefault(max(step, 0), []).append((fn, args))
+
+        for grp in range(1, len(GROUPS)):
+            first = max(STARTS[grp - 1] - 1, 0)
+            last = STARTS[grp] - 2
+            job(first, tables, grp)
+            for k in range(16):
+                job(first + k * (last - first + 1) // 16, stage_y, grp, k // 8, k % 8)
+        for grp in range(len(GROUPS)):
+            size = GROUPS[grp]
+            for b in range(4):
+                job(STARTS[grp] - (4 - b) * size // 8 if grp else 0, x_copy, grp, b)
+            for first in range(0, size, 4):
+                job(STARTS[grp] + 1 + first // 2, x_quant, grp, first, min(size, 4))
+
+        both = (0, 1)
         tables(0)
-        stage_y(0, 0)
-        stage_y(0, 1)
+        for l in both:
+            for h in range(8):
+                stage_y(0, l, h)
         stage_z(0)
-        stage_y(1, 0)
-        stage_y(1, 1)
-        for j in range(N_PAIRS + 11):
-            if j + 1 < N_PAIRS:
+        for j in range(NODES):
+            if j + 1 < NODES:
                 stage_z(j + 1)
-            if j < N_PAIRS:
+            if j < NODES:
                 stage_e(j)
-            fill = []
-            if j >= 10 and j - 10 < 32 and j <= N_PAIRS:
-                fill.append(("o", (j - 10) // 8, (j - 10) % 8))
-            if j + 2 < N_PAIRS:
-                fill.append(("y", j + 2, 0))
-                fill.append(("y", j + 2, 1))
+            fill = list(jobs.get(j, []))
+            if 3 <= j:
+                fill.insert(0, (node_o, (j - 3, both, j % 8 == 2)))
 
-            def take():
-                if fill:
-                    kind, a0, a1 = fill.pop(0)
-                    if kind == "o":
-                        node_o(a0, a1, False)
-                    else:
-                        stage_y(a0, a1)
+            def take(count):
+                for i in range(count):
+                    if fill:
+                        fn, args = fill.pop(0)
+                        fn(*args)
 
-            if 1 <= j <= N_PAIRS:
-                stage_tot(j - 1)
-                take()
-                stage_inv(j - 1)
-                take()
-                stage_n(j - 1)
-                stage_w(j - 1)
-                stage_c(j - 1)
-            take()
-            take()
-            take()
-            if j > N_PAIRS and j - 10 < 32:
-                node_o((j - 10) // 8, (j - 10) % 8, True)
-            if j >= 9:
-                grp, n = divmod(j - 9, 8)
-                if grp < 4:
-                    node_q(grp, n)
-            if j < N_PAIRS and 4 <= j % 8:
-                x_copy(j // 8, j % 8 - 4)
-            if 8 <= j <= N_PAIRS and j % 8 == 0:
-                x_quant(j // 8 - 1)
-            if (j + 3) % 8 == 0 and j + 3 < N_PAIRS:
-                tables((j + 3) // 8)
+            if 1 <= j:
+                stage_tot(j - 1, both)
+                take(1)
+                stage_inv(j - 1, both)
+                take(1)
+                stage_n(j - 1, both)
+                stage_w(j - 1, both)
+                stage_c(j - 1, both)
+            if 2 <= j:
+                node_q(j - 2, both)
+            take(len(fill))
+        last = NODES - 1
+        for l in both:
+            stage_tot(last, (l,))
+            stage_inv(last, (l,))
+            stage_n(last, (l,))
+            stage_w(last, (l,))
+            stage_c(last, (l,))
+            if l == 0:
+                node_o(last - 2, both, True)
+                node_q(last - 1, both)
+                node_o(last - 1, both, False)
+            node_q(last, (l,))
+            node_o(last, (l,), l == 0)

@@ -14,6 +14,7 @@ U8 = mybir.dt.uint8
 FP8X4 = mybir.dt.float8_e4m3fn_x4
 ALU = mybir.AluOpType
 ACTF = mybir.ActivationFunctionType
+ET = mybir.EngineType
 
 P = 128
 FLOPS = 2 * 32 * 512 * 512 * 128
@@ -21,8 +22,8 @@ FLOPS = 2 * 32 * 512 * 512 * 128
 PI_F32 = 3.1415927410125732
 
 NODES = 32
-GROUPS = (2, 2, 4, 8, 8, 8)
-STARTS = (0, 2, 4, 8, 16, 24)
+GROUPS = (2, 2, 4, 4, 4, 4, 4, 4, 4)
+STARTS = (0, 2, 4, 8, 12, 16, 20, 24, 28)
 
 
 def tile_polnormal_nolayer_kernel(tc, x, coords_x, coords_y, phis, dists_param, sigma_param, out):
@@ -41,7 +42,7 @@ def tile_polnormal_nolayer_kernel(tc, x, coords_x, coords_y, phis, dists_param, 
         sp = ctx.enter_context(tc.tile_pool(name="sp", bufs=3))
         xgp = ctx.enter_context(tc.tile_pool(name="xgp", bufs=2))
         cp = ctx.enter_context(tc.tile_pool(name="cp", bufs=3))
-        op = ctx.enter_context(tc.tile_pool(name="op", bufs=4))
+        op = ctx.enter_context(tc.tile_pool(name="op", bufs=8))
         pz = ctx.enter_context(tc.psum_pool(name="pz", bufs=4))
         ptp = ctx.enter_context(tc.psum_pool(name="ptp", bufs=2))
         pacc = ctx.enter_context(tc.psum_pool(name="pacc", bufs=2))
@@ -119,26 +120,27 @@ def tile_polnormal_nolayer_kernel(tc, x, coords_x, coords_y, phis, dists_param, 
         tqs = {}
         yts = {}
 
-        def tables(grp):
+        tparts = {}
+
+        def table_part(grp, part):
             size = GROUPS[grp]
             nodes = slice(STARTS[grp], STARTS[grp] + size)
             shape = [P, size, 4, 16]
-
-            def trig(row):
-                return cs[:, row, :].unsqueeze(1).unsqueeze(1).to_broadcast(shape)
-
-            def coord(row):
-                return cq[:, row, :, nodes].rearrange("q t o -> q o t").unsqueeze(3).to_broadcast(shape)
-
-            tx = tmp.tile(shape, F32, name="tx")
-            V.tensor_tensor(out=tx[:], in0=coord(0), in1=trig(1), op=ALU.mult)
-            ty = tmp.tile(shape, F32, name="ty")
-            V.tensor_tensor(out=ty[:], in0=coord(1), in1=trig(0), op=ALU.mult)
-            tq = tqp.tile(shape, F32, name="tq")
-            V.tensor_tensor(out=tq[:], in0=tx[:], in1=ty[:], op=ALU.add)
-            tqs[grp] = tq
-            y = yp.tile([P, size, 4, 2, 8, 16], F32, name="y")
-            yts[grp] = y
+            if part < 2:
+                prod = tmp.tile(shape, F32, name="prod%d" % part)
+                V.tensor_tensor(
+                    out=prod[:],
+                    in0=cq[:, part, :, nodes].rearrange("q t o -> q o t").unsqueeze(3).to_broadcast(shape),
+                    in1=cs[:, 1 - part, :].unsqueeze(1).unsqueeze(1).to_broadcast(shape),
+                    op=ALU.mult,
+                )
+                tparts[(grp, part)] = prod
+            else:
+                tq = tqp.tile(shape, F32, name="tq")
+                V.tensor_tensor(out=tq[:], in0=tparts[(grp, 0)][:], in1=tparts[(grp, 1)][:], op=ALU.add)
+                tqs[grp] = tq
+                y = yp.tile([P, size, 4, 2, 8, 16], F32, name="y")
+                yts[grp] = y
 
         def stage_y(grp, l, h):
             d = 2 * h + l
@@ -171,10 +173,12 @@ def tile_polnormal_nolayer_kernel(tc, x, coords_x, coords_y, phis, dists_param, 
 
         zs = {}
         gs = {}
+        sums = {}
         ws = {}
         tbs = {}
         wgs = {}
         accs = {}
+        codes = {}
         tots = {}
         invs = {}
 
@@ -182,10 +186,9 @@ def tile_polnormal_nolayer_kernel(tc, x, coords_x, coords_y, phis, dists_param, 
             grp = max(g for g in range(len(GROUPS)) if STARTS[g] <= o)
             return grp, o - STARTS[grp]
 
-        def stage_z(o):
+        def stage_z(o, ls):
             grp, n = group_of(o)
-            lst = []
-            for l in range(2):
+            for l in ls:
                 zb = pz.tile([P, 4, P], F32)
                 for t in range(4):
                     T.matmul(
@@ -196,27 +199,26 @@ def tile_polnormal_nolayer_kernel(tc, x, coords_x, coords_y, phis, dists_param, 
                         out=zb[:, t, :], lhsT=yts[grp][:, n, t, l].rearrange("q h p -> q (h p)"), rhs=ident[:],
                         is_transpose=True, start=False, stop=True,
                     )
-                lst.append(zb)
-            zs[o] = lst
+                zs[(o, l)] = zb
 
-        def stage_e(o):
-            ssum = sp.tile([P, 4], F32)
-            lst = []
-            for l in range(2):
-                for s in range(2):
-                    g = gp.tile([P, 512], F32)
-                    S.activation(
-                        out=g[:].rearrange("m (u q e) -> m u q e", u=2, e=2),
-                        in_=zs[o][l][:].rearrange("m (u e) q -> m u q e", e=2),
-                        func=ACTF.Exp,
-                        scale=nha[:, s : s + 1],
-                        accum_out=ssum[:, 2 * l + s : 2 * l + s + 1],
-                    )
-                    lst.append(g)
-            gs[o] = (ssum, lst)
+        def stage_e(o, l):
+            if l == 0:
+                ssum_new = sp.tile([P, 4], F32, name="ssum")
+                sums[o] = ssum_new
+            for s in range(2):
+                g = gp.tile([P, 512], F32)
+                c = 2 * l + s
+                S.activation(
+                    out=g[:].rearrange("m (u q e) -> m u q e", u=2, e=2),
+                    in_=zs[(o, l)][:].rearrange("m (u e) q -> m u q e", e=2),
+                    func=ACTF.Exp,
+                    scale=nha[:, s : s + 1],
+                    accum_out=sums[o][:, c : c + 1],
+                )
+                gs[(o, l, s)] = g
 
         def stage_tot(o, ls):
-            ssum = gs[o][0]
+            ssum = sums[o]
             tot = sp.tile([P, 2 * len(ls)], F32)
             V.tensor_scalar(
                 out=tot[:], in0=ssum[:, 2 * ls[0] : 2 * ls[-1] + 2], scalar1=1e-20, scalar2=None, op0=ALU.add
@@ -236,7 +238,7 @@ def tile_polnormal_nolayer_kernel(tc, x, coords_x, coords_y, phis, dists_param, 
                 for s in range(2):
                     w = wp.tile([P, 512], BF16)
                     V.tensor_scalar(
-                        out=w[:], in0=gs[o][1][2 * l + s][:], scalar1=invs[(o, l, s)], scalar2=None, op0=ALU.mult
+                        out=w[:], in0=gs[(o, l, s)][:], scalar1=invs[(o, l, s)], scalar2=None, op0=ALU.mult
                     )
                     ws[(o, l, s)] = w
 
@@ -265,8 +267,12 @@ def tile_polnormal_nolayer_kernel(tc, x, coords_x, coords_y, phis, dists_param, 
             V.quantize_mx(
                 out=wc[:, cols].bitcast(FP8X4), scales=wsc[:, cols], in_=wgs[o][:, 512 * first : 512 * last]
             )
+            codes[(o, ls)] = (wc, wsc)
+
+        def node_m(o, ls):
+            wc, wsc = codes[(o, ls)]
             acc = pacc.tile([P, 512], F32)
-            for i in range(first, last):
+            for i in range(2 * ls[0], 2 * ls[-1] + 2):
                 mc = slice(P * i, P * i + P)
                 oc = slice(P * o, P * o + P)
                 T.matmul_mx(
@@ -300,32 +306,28 @@ def tile_polnormal_nolayer_kernel(tc, x, coords_x, coords_y, phis, dists_param, 
             jobs.setdefault(max(step, 0), []).append((fn, args))
 
         for grp in range(1, len(GROUPS)):
-            first = max(STARTS[grp - 1] - 1, 0)
-            last = STARTS[grp] - 2
-            job(first, tables, grp)
+            steps = GROUPS[grp - 1]
+            first = STARTS[grp] - 1 - steps
+            for part in range(3):
+                job(first - 2 + part, table_part, grp, part)
             for k in range(16):
-                job(first + k * (last - first + 1) // 16, stage_y, grp, k // 8, k % 8)
+                job(first + k * steps // 16, stage_y, grp, k // 8, k % 8)
         for grp in range(len(GROUPS)):
             size = GROUPS[grp]
             for b in range(4):
-                job(STARTS[grp] - (4 - b) * size // 8 if grp else 0, x_copy, grp, b)
-            for first in range(0, size, 4):
-                job(STARTS[grp] + 1 + first // 2, x_quant, grp, first, min(size, 4))
+                job(STARTS[grp] + 3 - size + b * size // 4, x_copy, grp, b)
+            job(STARTS[grp] + 2, x_quant, grp, 0, size)
 
         both = (0, 1)
-        tables(0)
+        for part in range(3):
+            table_part(0, part)
         for l in both:
             for h in range(8):
                 stage_y(0, l, h)
-        stage_z(0)
+        stage_z(0, both)
+        ctx.enter_context(tc.manual_schedule(engines={ET.PE, ET.Activation, ET.DVE}))
         for j in range(NODES):
-            if j + 1 < NODES:
-                stage_z(j + 1)
-            if j < NODES:
-                stage_e(j)
             fill = list(jobs.get(j, []))
-            if 3 <= j:
-                fill.insert(0, (node_o, (j - 3, both, j % 8 == 2)))
 
             def take(count):
                 for i in range(count):
@@ -333,27 +335,50 @@ def tile_polnormal_nolayer_kernel(tc, x, coords_x, coords_y, phis, dists_param, 
                         fn, args = fill.pop(0)
                         fn(*args)
 
-            if 1 <= j:
+            for l in both:
+                stage_e(j, l)
+                if j >= 2:
+                    stage_c(j - 2, (l,))
+            if j >= 4:
+                node_o(j - 4, both, j % 4 == 3)
+            if j >= 3:
+                node_q(j - 3, both)
+            if j + 1 < NODES:
+                stage_z(j + 1, (0,))
+            if j >= 3:
+                node_m(j - 3, both)
+            if j + 1 < NODES:
+                stage_z(j + 1, (1,))
+            if j >= 1:
                 stage_tot(j - 1, both)
                 take(1)
                 stage_inv(j - 1, both)
                 take(1)
                 stage_n(j - 1, both)
                 stage_w(j - 1, both)
-                stage_c(j - 1, both)
-            if 2 <= j:
-                node_q(j - 2, both)
             take(len(fill))
         last = NODES - 1
+        stage_tot(last, (0,))
+        stage_inv(last, (0,))
+        stage_n(last, (0,))
+        stage_c(last - 1, (0,))
+        stage_w(last, (0,))
+        stage_tot(last, (1,))
+        stage_inv(last, (1,))
+        stage_n(last, (1,))
+        stage_c(last - 1, (1,))
+        stage_w(last, (1,))
+        node_q(last - 2, both)
+        node_m(last - 2, both)
+        node_q(last - 1, both)
+        stage_c(last, (0,))
+        node_o(last - 3, both, False)
+        node_m(last - 1, both)
+        stage_c(last, (1,))
+        node_o(last - 2, both, True)
         for l in both:
-            stage_tot(last, (l,))
-            stage_inv(last, (l,))
-            stage_n(last, (l,))
-            stage_w(last, (l,))
-            stage_c(last, (l,))
-            if l == 0:
-                node_o(last - 2, both, True)
-                node_q(last - 1, both)
-                node_o(last - 1, both, False)
             node_q(last, (l,))
+        node_o(last - 1, both, True)
+        for l in both:
+            node_m(last, (l,))
             node_o(last, (l,), l == 0)

@@ -35,7 +35,7 @@ def tile_polnormal_nolayer_kernel(tc, x, coords_x, coords_y, phis, dists_param, 
         const = ctx.enter_context(tc.tile_pool(name="const", bufs=1))
         tmp = ctx.enter_context(tc.tile_pool(name="tmp", bufs=2))
         tqp = ctx.enter_context(tc.tile_pool(name="tqp", bufs=2))
-        yp = ctx.enter_context(tc.tile_pool(name="yp", bufs=3))
+        yp = ctx.enter_context(tc.tile_pool(name="yp", bufs=2))
         wgp = ctx.enter_context(tc.tile_pool(name="wgp", bufs=3))
         gp = ctx.enter_context(tc.tile_pool(name="gp", bufs=10))
         wp = ctx.enter_context(tc.tile_pool(name="wp", bufs=8))
@@ -75,6 +75,7 @@ def tile_polnormal_nolayer_kernel(tc, x, coords_x, coords_y, phis, dists_param, 
         identp = const.tile([P, P], F32)
         V.tensor_copy(out=identp[:].rearrange("k (p h) -> k p h", h=8), in_=ident[:].rearrange("k (h p) -> k p h", p=16))
 
+        ctx.enter_context(tc.manual_schedule(engines={ET.PE, ET.Activation, ET.DVE}))
         warm = const.tile([P, 1], F32)
         V.memset(warm[:], 0.0)
         S.activation(out=warm[:], in_=warm[:], func=ACTF.Silu)
@@ -94,28 +95,26 @@ def tile_polnormal_nolayer_kernel(tc, x, coords_x, coords_y, phis, dists_param, 
         pcv = pc[:, :, 0:64].rearrange("q t (a o) -> q a t o", a=2)
         p2 = const.tile([P, 2, 16], F32)
         V.scalar_tensor_tensor(out=p2[:], in0=qi[:], scalar=-2.0 * math.pi, in1=ph[:], op0=ALU.mult, op1=ALU.add)
-        cq = const.tile([P, 2, 4, 32], F32)
-        S.copy(out=cq[:], in_=pcv)
         ang = const.tile([P, 2, 16], F32)
         V.tensor_scalar(out=ang[:], in0=p2[:], scalar1=-PI_F32, scalar2=PI_F32, op0=ALU.max, op1=ALU.min)
-        dm2 = const.tile([P, 16], F32)
-        V.tensor_scalar(out=dm2[:], in0=th[:, 0:16], scalar1=1.0, scalar2=-2.0, op0=ALU.add, op1=ALU.mult)
         cs = const.tile([P, 2, 16], F32)
         S.activation(out=cs[:], in_=ang[:], func=ACTF.Sin)
+        cq = const.tile([P, 2, 4, 32], F32)
+        V.tensor_copy(out=cq[:], in_=pcv)
+        sq = const.tile([P, 2, 4, 32], F32)
+        S.activation(out=sq[:], in_=cq[:], func=ACTF.Square)
+        warm_exp = const.tile([P, 1], F32)
+        S.activation(out=warm_exp[:], in_=warm[:], func=ACTF.Exp)
+        dm2 = const.tile([P, 16], F32)
+        V.tensor_scalar(out=dm2[:], in0=th[:, 0:16], scalar1=1.0, scalar2=-2.0, op0=ALU.add, op1=ALU.mult)
         dd = const.tile([P, 16], F32)
         V.tensor_scalar(out=dd[:], in0=th[:, 0:16], scalar1=1.0, scalar2=None, op0=ALU.add)
-        sq = const.tile([P, 2, 4, 32], F32)
-        S.activation(out=sq[:], in_=pcv, func=ACTF.Square)
-        sg = const.tile([P, 2], F32)
-        V.tensor_scalar(out=sg[:], in0=th[:, 16:18], scalar1=1.0, scalar2=1e-10, op0=ALU.add, op1=ALU.max)
         dsq = const.tile([P, 16], F32)
         V.tensor_tensor(out=dsq[:], in0=dd[:], in1=dd[:], op=ALU.mult)
-        sgm = const.tile([P, 2], F32)
-        V.scalar_tensor_tensor(out=sgm[:], in0=sg[:], scalar=-2.0, in1=sg[:], op0=ALU.mult, op1=ALU.mult)
-        nha = const.tile([P, 2], F32)
-        V.reciprocal(out=nha[:], in_=sgm[:])
         r2q = const.tile([P, 4, 32], F32)
-        V.tensor_tensor(out=r2q[:], in0=sq[:, 0], in1=sq[:, 1], op=ALU.add)
+        sg = const.tile([P, 2], F32)
+        sgm = const.tile([P, 2], F32)
+        nha = const.tile([P, 2], F32)
 
         tqs = {}
         yts = {}
@@ -189,7 +188,7 @@ def tile_polnormal_nolayer_kernel(tc, x, coords_x, coords_y, phis, dists_param, 
         def stage_z(o, ls):
             grp, n = group_of(o)
             for l in ls:
-                zb = pz.tile([P, 4, P], F32)
+                zb = pz.tile([P, 4, P], F32, tag="zb")
                 for t in range(4):
                     T.matmul(
                         out=zb[:, t, :], lhsT=r2q[:, t, o : o + 1].to_broadcast([P, P]), rhs=ident[:], is_transpose=True,
@@ -242,9 +241,12 @@ def tile_polnormal_nolayer_kernel(tc, x, coords_x, coords_y, phis, dists_param, 
                     )
                     ws[(o, l, s)] = w
 
-        def stage_w(o, ls):
+        def stage_w(o, ls, pool):
             for l in ls:
-                tb = ptp.tile([P, 2, 2, P], F32, tag="tp")
+                if pool is ptp:
+                    tb = ptp.tile([P, 2, 2, P], F32, tag="tp")
+                else:
+                    tb = pz.tile([P, 2, 2, P], F32, tag="zb")
                 for s in range(2):
                     words = ws[(o, l, s)][:].bitcast(F32)
                     for u in range(2):
@@ -269,9 +271,9 @@ def tile_polnormal_nolayer_kernel(tc, x, coords_x, coords_y, phis, dists_param, 
             )
             codes[(o, ls)] = (wc, wsc)
 
-        def node_m(o, ls):
+        def node_m(o, ls, pool):
             wc, wsc = codes[(o, ls)]
-            acc = pacc.tile([P, 512], F32)
+            acc = pool.tile([P, 512], F32, tag="zb" if pool is pz else "acc")
             for i in range(2 * ls[0], 2 * ls[-1] + 2):
                 mc = slice(P * i, P * i + P)
                 oc = slice(P * o, P * o + P)
@@ -316,16 +318,23 @@ def tile_polnormal_nolayer_kernel(tc, x, coords_x, coords_y, phis, dists_param, 
             size = GROUPS[grp]
             for b in range(4):
                 job(STARTS[grp] + 3 - size + b * size // 4, x_copy, grp, b)
-            job(STARTS[grp] + 2, x_quant, grp, 0, size)
+            for n in range(0, size, 4):
+                job(STARTS[grp] + 2 + n // 2, x_quant, grp, n, min(size, 4))
 
         both = (0, 1)
+        last = NODES - 1
         for part in range(3):
             table_part(0, part)
-        for l in both:
-            for h in range(8):
-                stage_y(0, l, h)
-        stage_z(0, both)
-        ctx.enter_context(tc.manual_schedule(engines={ET.PE, ET.Activation, ET.DVE}))
+        V.tensor_tensor(out=r2q[:], in0=sq[:, 0], in1=sq[:, 1], op=ALU.add)
+        for h in range(8):
+            stage_y(0, 0, h)
+        stage_z(0, (0,))
+        V.tensor_scalar(out=sg[:], in0=th[:, 16:18], scalar1=1.0, scalar2=1e-10, op0=ALU.add, op1=ALU.max)
+        V.scalar_tensor_tensor(out=sgm[:], in0=sg[:], scalar=-2.0, in1=sg[:], op0=ALU.mult, op1=ALU.mult)
+        V.reciprocal(out=nha[:], in_=sgm[:])
+        for h in range(8):
+            stage_y(0, 1, h)
+        stage_z(0, (1,))
         for j in range(NODES):
             fill = list(jobs.get(j, []))
 
@@ -335,19 +344,23 @@ def tile_polnormal_nolayer_kernel(tc, x, coords_x, coords_y, phis, dists_param, 
                         fn, args = fill.pop(0)
                         fn(*args)
 
-            for l in both:
-                stage_e(j, l)
-                if j >= 2:
-                    stage_c(j - 2, (l,))
-            if j >= 4:
-                node_o(j - 4, both, j % 4 == 3)
+            stage_e(j, 0)
+            if j >= 2:
+                stage_c(j - 2, (0,))
+            if j == last:
+                stage_c(j - 2, (1,))
+            stage_e(j, 1)
+            if 2 <= j < last:
+                stage_c(j - 2, (1,))
+            if 4 <= j < last:
+                node_o(j - 4, both, j % 2 == 1 or j < 10)
             if j >= 3:
                 node_q(j - 3, both)
-            if j + 1 < NODES:
+            if j < last:
                 stage_z(j + 1, (0,))
             if j >= 3:
-                node_m(j - 3, both)
-            if j + 1 < NODES:
+                node_m(j - 3, both, pacc)
+            if j < last:
                 stage_z(j + 1, (1,))
             if j >= 1:
                 stage_tot(j - 1, both)
@@ -355,30 +368,26 @@ def tile_polnormal_nolayer_kernel(tc, x, coords_x, coords_y, phis, dists_param, 
                 stage_inv(j - 1, both)
                 take(1)
                 stage_n(j - 1, both)
-                stage_w(j - 1, both)
+                stage_w(j - 1, both, ptp)
             take(len(fill))
-        last = NODES - 1
-        stage_tot(last, (0,))
-        stage_inv(last, (0,))
-        stage_n(last, (0,))
-        stage_c(last - 1, (0,))
-        stage_w(last, (0,))
-        stage_tot(last, (1,))
-        stage_inv(last, (1,))
-        stage_n(last, (1,))
-        stage_c(last - 1, (1,))
-        stage_w(last, (1,))
+        for l in both:
+            stage_tot(last, (l,))
+            stage_inv(last, (l,))
+            stage_n(last, (l,))
+            stage_w(last, (l,), pz)
         node_q(last - 2, both)
-        node_m(last - 2, both)
-        node_q(last - 1, both)
+        node_o(last - 4, both, False)
+        node_m(last - 2, both, pacc)
+        stage_c(last - 1, both)
         stage_c(last, (0,))
-        node_o(last - 3, both, False)
-        node_m(last - 1, both)
+        node_q(last - 1, both)
         stage_c(last, (1,))
-        node_o(last - 2, both, True)
+        node_o(last - 3, both, True)
+        node_m(last - 1, both, pacc)
         for l in both:
             node_q(last, (l,))
+            node_m(last, (l,), pz)
+        node_o(last - 2, both, True)
         node_o(last - 1, both, True)
-        for l in both:
-            node_m(last, (l,))
-            node_o(last, (l,), l == 0)
+        node_o(last, (0,), True)
+        node_o(last, (1,), False)

@@ -36,24 +36,26 @@ def tile_polnormal_nolayer_kernel(tc, x, coords_x, coords_y, phis, dists_param, 
         tmp = ctx.enter_context(tc.tile_pool(name="tmp", bufs=2))
         tqp = ctx.enter_context(tc.tile_pool(name="tqp", bufs=2))
         yp = ctx.enter_context(tc.tile_pool(name="yp", bufs=2))
-        wgp = ctx.enter_context(tc.tile_pool(name="wgp", bufs=3))
-        gp = ctx.enter_context(tc.tile_pool(name="gp", bufs=10))
-        wp = ctx.enter_context(tc.tile_pool(name="wp", bufs=8))
+        wgp = ctx.enter_context(tc.tile_pool(name="wgp", bufs=4))
+        gp = ctx.enter_context(tc.tile_pool(name="gp", bufs=14))
+        wp = ctx.enter_context(tc.tile_pool(name="wp", bufs=10))
         sp = ctx.enter_context(tc.tile_pool(name="sp", bufs=3))
-        xgp = ctx.enter_context(tc.tile_pool(name="xgp", bufs=2))
-        cp = ctx.enter_context(tc.tile_pool(name="cp", bufs=3))
+        xgp = ctx.enter_context(tc.tile_pool(name="xgp", bufs=3))
+        cp = ctx.enter_context(tc.tile_pool(name="cp", bufs=4))
         op = ctx.enter_context(tc.tile_pool(name="op", bufs=8))
-        pz = ctx.enter_context(tc.psum_pool(name="pz", bufs=4))
-        ptp = ctx.enter_context(tc.psum_pool(name="ptp", bufs=2))
+        pz = ctx.enter_context(tc.psum_pool(name="pz", bufs=3))
+        ptp = ctx.enter_context(tc.psum_pool(name="ptp", bufs=3))
         pacc = ctx.enter_context(tc.psum_pool(name="pacc", bufs=2))
         ctx.enter_context(nc.allow_non_contiguous_dma(reason="rows of 256 and 512 bytes"))
 
-        pv = const.tile([P, 64], BF16)
+        pa = const.tile([P, 16], BF16)
+        V.memset(pa[:].bitcast(I32), 0)
+        pv = const.tile([P, 32], BF16)
         V.memset(pv[:].bitcast(I32), 0)
         cn = const.tile([P, 512], BF16)
-        nc.sync.dma_start(out=pv[0:1, 0:16], in_=phis.unsqueeze(0))
-        nc.sync.dma_start(out=pv[0:1, 16:32], in_=dists_param.unsqueeze(0))
-        nc.sync.dma_start(out=pv[0:1, 32:34], in_=sigma_param.unsqueeze(0))
+        nc.sync.dma_start(out=pa[0:1, :], in_=phis.unsqueeze(0))
+        nc.sync.dma_start(out=pv[0:1, 0:16], in_=dists_param.unsqueeze(0))
+        nc.sync.dma_start(out=pv[0:1, 16:18], in_=sigma_param.unsqueeze(0))
         nc.sync.dma_start(out=cn[0:32, :], in_=coords_x.rearrange("a o i j -> (a o) (i j)"))
         nc.sync.dma_start(out=cn[32:64, :], in_=coords_y.rearrange("a o i j -> (a o) (i j)"))
         V.memset(cn[64:128, :].bitcast(I32), 0)
@@ -79,24 +81,29 @@ def tile_polnormal_nolayer_kernel(tc, x, coords_x, coords_y, phis, dists_param, 
         warm = const.tile([P, 1], F32)
         V.memset(warm[:], 0.0)
         S.activation(out=warm[:], in_=warm[:], func=ACTF.Silu)
-        pp = ptp.tile([P, 64], F32, tag="tp")
-        T.matmul(out=pp[:], lhsT=ones[:], rhs=pv[:], start=True, stop=True)
-        ph = const.tile([P, 2, 16], F32)
-        V.tensor_scalar(out=ph[:, 1, :], in0=pp[:, 0:16], scalar1=0.5 * math.pi, scalar2=None, op0=ALU.add)
-        V.tensor_copy(out=ph[:, 0, :], in_=pp[:, 0:16])
-        th = const.tile([P, 18], F32)
-        S.activation(out=th[:], in_=pp[:, 16:34], func=ACTF.Tanh, scale=0.5)
+        pp = ptp.tile([P, 16], F32, tag="tp")
+        T.matmul(out=pp[:], lhsT=ones[:], rhs=pa[:], start=True, stop=True)
+        pq = pacc.tile([P, 32], F32, tag="acc")
+        T.matmul(out=pq[:], lhsT=ones[:], rhs=pv[:], start=True, stop=True)
+        turn = 2.0 * math.pi
         qi = const.tile([P, 2, 16], I32)
-        V.tensor_scalar(out=qi[:], in0=ph[:], scalar1=1.0 / (2.0 * math.pi), scalar2=None, op0=ALU.mult)
+        V.tensor_scalar(out=qi[:, 0, :], in0=pp[:], scalar1=1.0 / turn, scalar2=None, op0=ALU.mult)
+        V.tensor_scalar(out=qi[:, 1, :], in0=pp[:], scalar1=1.0 / turn, scalar2=0.25, op0=ALU.mult, op1=ALU.add)
+        th = const.tile([P, 18], F32)
+        S.activation(out=th[:], in_=pq[:, 0:18], func=ACTF.Tanh, scale=0.5)
         pc = ptp.tile([P, 4, P], BF16, tag="tp")
         cells = cn[:].rearrange("r (q t) -> r t q", t=4)
         for t in range(4):
             T.transpose(out=pc[:, t, :], in_=cells[:, t, :], identity=identb[:])
         pcv = pc[:, :, 0:64].rearrange("q t (a o) -> q a t o", a=2)
         p2 = const.tile([P, 2, 16], F32)
-        V.scalar_tensor_tensor(out=p2[:], in0=qi[:], scalar=-2.0 * math.pi, in1=ph[:], op0=ALU.mult, op1=ALU.add)
+        for row in range(2):
+            V.scalar_tensor_tensor(
+                out=p2[:, row, :], in0=qi[:, row, :], scalar=-turn, in1=pp[:], op0=ALU.mult, op1=ALU.add
+            )
         ang = const.tile([P, 2, 16], F32)
-        V.tensor_scalar(out=ang[:], in0=p2[:], scalar1=-PI_F32, scalar2=PI_F32, op0=ALU.max, op1=ALU.min)
+        V.tensor_scalar(out=ang[:, 0, :], in0=p2[:, 0, :], scalar1=-PI_F32, scalar2=PI_F32, op0=ALU.max, op1=ALU.min)
+        V.tensor_scalar(out=ang[:, 1, :], in0=p2[:, 1, :], scalar1=0.5 * math.pi, scalar2=PI_F32, op0=ALU.add, op1=ALU.min)
         cs = const.tile([P, 2, 16], F32)
         S.activation(out=cs[:], in_=ang[:], func=ACTF.Sin)
         cq = const.tile([P, 2, 4, 32], F32)
@@ -201,12 +208,13 @@ def tile_polnormal_nolayer_kernel(tc, x, coords_x, coords_y, phis, dists_param, 
                 zs[(o, l)] = zb
 
         def stage_e(o, l):
-            if l == 0:
-                ssum_new = sp.tile([P, 4], F32, name="ssum")
+            if l == 0 and o % 2 == 0:
+                ssum_new = sp.tile([P, 8], F32, name="ssum")
                 sums[o] = ssum_new
+                sums[o + 1] = ssum_new
             for s in range(2):
                 g = gp.tile([P, 512], F32)
-                c = 2 * l + s
+                c = 4 * (o % 2) + 2 * l + s
                 S.activation(
                     out=g[:].rearrange("m (u q e) -> m u q e", u=2, e=2),
                     in_=zs[(o, l)][:].rearrange("m (u e) q -> m u q e", e=2),
@@ -216,21 +224,21 @@ def tile_polnormal_nolayer_kernel(tc, x, coords_x, coords_y, phis, dists_param, 
                 )
                 gs[(o, l, s)] = g
 
-        def stage_tot(o, ls):
-            ssum = sums[o]
-            tot = sp.tile([P, 2 * len(ls)], F32)
+        def stage_tot(parts):
+            first = 4 * (parts[0][0] % 2) + 2 * parts[0][1]
+            tot = sp.tile([P, 2 * len(parts)], F32)
             V.tensor_scalar(
-                out=tot[:], in0=ssum[:, 2 * ls[0] : 2 * ls[-1] + 2], scalar1=1e-20, scalar2=None, op0=ALU.add
+                out=tot[:], in0=sums[parts[0][0]][:, first : first + 2 * len(parts)], scalar1=1e-20, scalar2=None,
+                op0=ALU.add,
             )
-            tots[o] = tot
+            tots[parts] = tot
 
-        def stage_inv(o, ls):
-            inv = sp.tile([P, 2 * len(ls)], F32)
-            V.reciprocal(out=inv[:], in_=tots[o][:])
-            for l in ls:
-                for s in range(2):
-                    c = 2 * (l - ls[0]) + s
-                    invs[(o, l, s)] = inv[:, c : c + 1]
+        def stage_inv(parts):
+            inv = sp.tile([P, 2 * len(parts)], F32)
+            V.reciprocal(out=inv[:], in_=tots[parts][:])
+            for c in range(2 * len(parts)):
+                o, l = parts[c // 2]
+                invs[(o, l, c % 2)] = inv[:, c : c + 1]
 
         def stage_n(o, ls):
             for l in ls:
@@ -319,7 +327,7 @@ def tile_polnormal_nolayer_kernel(tc, x, coords_x, coords_y, phis, dists_param, 
             for b in range(4):
                 job(STARTS[grp] + 3 - size + b * size // 4, x_copy, grp, b)
             for n in range(0, size, 4):
-                job(STARTS[grp] + 2 + n // 2, x_quant, grp, n, min(size, 4))
+                job(STARTS[grp] + 3 - 1 + n // 2, x_quant, grp, n, min(size, 4))
 
         both = (0, 1)
         last = NODES - 1
@@ -328,9 +336,11 @@ def tile_polnormal_nolayer_kernel(tc, x, coords_x, coords_y, phis, dists_param, 
         V.tensor_tensor(out=r2q[:], in0=sq[:, 0], in1=sq[:, 1], op=ALU.add)
         for h in range(8):
             stage_y(0, 0, h)
+            if h == 1:
+                V.tensor_scalar(out=sg[:], in0=th[:, 16:18], scalar1=1.0, scalar2=1e-10, op0=ALU.add, op1=ALU.max)
+            if h == 4:
+                V.scalar_tensor_tensor(out=sgm[:], in0=sg[:], scalar=-2.0, in1=sg[:], op0=ALU.mult, op1=ALU.mult)
         stage_z(0, (0,))
-        V.tensor_scalar(out=sg[:], in0=th[:, 16:18], scalar1=1.0, scalar2=1e-10, op0=ALU.add, op1=ALU.max)
-        V.scalar_tensor_tensor(out=sgm[:], in0=sg[:], scalar=-2.0, in1=sg[:], op0=ALU.mult, op1=ALU.mult)
         V.reciprocal(out=nha[:], in_=sgm[:])
         for h in range(8):
             stage_y(0, 1, h)
@@ -345,49 +355,65 @@ def tile_polnormal_nolayer_kernel(tc, x, coords_x, coords_y, phis, dists_param, 
                         fn(*args)
 
             stage_e(j, 0)
-            if j >= 2:
-                stage_c(j - 2, (0,))
-            if j == last:
-                stage_c(j - 2, (1,))
-            stage_e(j, 1)
-            if 2 <= j < last:
-                stage_c(j - 2, (1,))
-            if 4 <= j < last:
-                node_o(j - 4, both, j % 2 == 1 or j < 10)
             if j >= 3:
-                node_q(j - 3, both)
+                stage_c(j - 3, (0,))
+            if j == last:
+                stage_c(j - 3, (1,))
+            stage_e(j, 1)
+            if 3 <= j < last:
+                stage_c(j - 3, (1,))
+            if j >= 7 and j % 2 == 1:
+                node_o(j - 6, both, j < 14 or j % 4 == 3)
             if j < last:
                 stage_z(j + 1, (0,))
-            if j >= 3:
-                node_m(j - 3, both, pacc)
-            if j < last:
                 stage_z(j + 1, (1,))
-            if j >= 1:
-                stage_tot(j - 1, both)
-                take(1)
-                stage_inv(j - 1, both)
-                take(1)
-                stage_n(j - 1, both)
-                stage_w(j - 1, both, ptp)
+            if j >= 6 and j % 2 == 0:
+                node_m(j - 6, both, pacc)
+                node_m(j - 5, both, pacc)
+            if j >= 2:
+                if j % 2 == 0:
+                    pair = ((j - 2, 0), (j - 2, 1), (j - 1, 0), (j - 1, 1))
+                    stage_tot(pair)
+                    take(2)
+                    stage_inv(pair)
+                    take(2)
+                stage_n(j - 2, both)
+                stage_w(j - 2, both, ptp)
+            if j >= 4:
+                node_q(j - 4, both)
+            if j >= 7 and j % 2 == 1:
+                node_o(j - 7, both, False)
             take(len(fill))
-        for l in both:
-            stage_tot(last, (l,))
-            stage_inv(last, (l,))
-            stage_n(last, (l,))
-            stage_w(last, (l,), pz)
-        node_q(last - 2, both)
-        node_o(last - 4, both, False)
-        node_m(last - 2, both, pacc)
+        node_m(last - 5, both, pacc)
+        node_m(last - 4, both, pacc)
+
+        def finish(parts):
+            stage_tot(parts)
+            stage_inv(parts)
+            for o, l in parts:
+                stage_n(o, (l,))
+                stage_w(o, (l,), pz)
+
+        finish(((last - 1, 0), (last - 1, 1)))
+        stage_c(last - 2, both)
+        node_o(last - 5, both, True)
+        node_o(last - 4, both, True)
+        finish(((last, 0),))
+        node_q(last - 3, both)
+        node_m(last - 3, both, pacc)
+        finish(((last, 1),))
         stage_c(last - 1, both)
+        node_q(last - 2, both)
+        node_m(last - 2, both, pacc)
+        node_o(last - 3, both, True)
         stage_c(last, (0,))
         node_q(last - 1, both)
-        stage_c(last, (1,))
-        node_o(last - 3, both, True)
         node_m(last - 1, both, pacc)
+        stage_c(last, (1,))
         for l in both:
             node_q(last, (l,))
             node_m(last, (l,), pz)
         node_o(last - 2, both, True)
-        node_o(last - 1, both, True)
+        node_o(last - 1, both, False)
         node_o(last, (0,), True)
         node_o(last, (1,), False)

@@ -355,21 +355,18 @@ def tile_polnormal_nolayer_kernel(tc, x, coords_x, coords_y, phis, dists_param, 
                         fn(*args)
 
             stage_e(j, 0)
-            if j >= 3:
-                stage_c(j - 3, (0,))
-            if j == last:
-                stage_c(j - 3, (1,))
             stage_e(j, 1)
-            if 3 <= j < last:
-                stage_c(j - 3, (1,))
+            if j >= 3:
+                stage_c(j - 3, both)
             if j >= 7 and j % 2 == 1:
                 node_o(j - 6, both, j < 14 or j % 4 == 3)
             if j < last:
                 stage_z(j + 1, (0,))
-                stage_z(j + 1, (1,))
             if j >= 6 and j % 2 == 0:
                 node_m(j - 6, both, pacc)
                 node_m(j - 5, both, pacc)
+            if j < last:
+                stage_z(j + 1, (1,))
             if j >= 2:
                 if j % 2 == 0:
                     pair = ((j - 2, 0), (j - 2, 1), (j - 1, 0), (j - 1, 1))

@@ -281,7 +281,7 @@ def tile_polnormal_nolayer_kernel(tc, x, coords_x, coords_y, phis, dists_param, 
 
         def node_m(o, ls, pool):
             wc, wsc = codes[(o, ls)]
-            acc = pool.tile([P, 512], F32, tag="zb" if pool is pz else "acc")
+            acc = pool.tile([P, 512], F32, tag="zb" if pool is pz else "tp" if pool is ptp else "acc")
             for i in range(2 * ls[0], 2 * ls[-1] + 2):
                 mc = slice(P * i, P * i + P)
                 oc = slice(P * o, P * o + P)
@@ -319,7 +319,7 @@ def tile_polnormal_nolayer_kernel(tc, x, coords_x, coords_y, phis, dists_param, 
             steps = GROUPS[grp - 1]
             first = STARTS[grp] - 1 - steps
             for part in range(3):
-                job(first - 2 + part, table_part, grp, part)
+                job(first - 3 + part, table_part, grp, part)
             for k in range(16):
                 job(first + k * steps // 16, stage_y, grp, k // 8, k % 8)
         for grp in range(len(GROUPS)):
@@ -327,7 +327,7 @@ def tile_polnormal_nolayer_kernel(tc, x, coords_x, coords_y, phis, dists_param, 
             for b in range(4):
                 job(STARTS[grp] + 3 - size + b * size // 4, x_copy, grp, b)
             for n in range(0, size, 4):
-                job(STARTS[grp] + 3 - 1 + n // 2, x_quant, grp, n, min(size, 4))
+                job(STARTS[grp] + 3 + n // 2, x_quant, grp, n, min(size, 4))
 
         both = (0, 1)
         last = NODES - 1
@@ -359,7 +359,7 @@ def tile_polnormal_nolayer_kernel(tc, x, coords_x, coords_y, phis, dists_param, 
             if j >= 3:
                 stage_c(j - 3, both)
             if j >= 7 and j % 2 == 1:
-                node_o(j - 6, both, j < 14 or j % 4 == 3)
+                node_o(j - 6, both, j % 8 == 7 or j < 10)
             if j < last:
                 stage_z(j + 1, (0,))
             if j >= 6 and j % 2 == 0:
@@ -376,40 +376,45 @@ def tile_polnormal_nolayer_kernel(tc, x, coords_x, coords_y, phis, dists_param, 
                     take(2)
                 stage_n(j - 2, both)
                 stage_w(j - 2, both, ptp)
+            if j == last:
+                stage_tot(((last - 1, 0), (last - 1, 1)))
             if j >= 4:
                 node_q(j - 4, both)
+            if j == last:
+                stage_inv(((last - 1, 0), (last - 1, 1)))
             if j >= 7 and j % 2 == 1:
                 node_o(j - 7, both, False)
             take(len(fill))
         node_m(last - 5, both, pacc)
         node_m(last - 4, both, pacc)
-
-        def finish(parts):
-            stage_tot(parts)
-            stage_inv(parts)
-            for o, l in parts:
-                stage_n(o, (l,))
-                stage_w(o, (l,), pz)
-
-        finish(((last - 1, 0), (last - 1, 1)))
+        stage_n(last - 1, (0,))
+        stage_w(last - 1, (0,), pz)
+        stage_tot(((last, 0),))
+        stage_n(last - 1, (1,))
+        stage_w(last - 1, (1,), pz)
+        stage_inv(((last, 0),))
         stage_c(last - 2, both)
-        node_o(last - 5, both, True)
         node_o(last - 4, both, True)
-        finish(((last, 0),))
         node_q(last - 3, both)
-        node_m(last - 3, both, pacc)
-        finish(((last, 1),))
+        stage_tot(((last, 1),))
+        stage_n(last, (0,))
+        stage_w(last, (0,), pz)
+        node_m(last - 3, both, ptp)
+        stage_inv(((last, 1),))
+        node_o(last - 5, both, False)
+        stage_n(last, (1,))
+        stage_w(last, (1,), ptp)
         stage_c(last - 1, both)
         node_q(last - 2, both)
-        node_m(last - 2, both, pacc)
-        node_o(last - 3, both, True)
+        node_m(last - 2, both, ptp)
         stage_c(last, (0,))
         node_q(last - 1, both)
-        node_m(last - 1, both, pacc)
+        node_m(last - 1, both, pz)
         stage_c(last, (1,))
         for l in both:
             node_q(last, (l,))
             node_m(last, (l,), pz)
+        node_o(last - 3, both, True)
         node_o(last - 2, both, True)
         node_o(last - 1, both, False)
         node_o(last, (0,), True)

import math
from contextlib import ExitStack

import concourse.bass as bass
import concourse.mybir as mybir
import concourse.tile as tile
from concourse.masks import make_identity

F32 = mybir.dt.float32
BF16 = mybir.dt.bfloat16
I32 = mybir.dt.int32
U32 = mybir.dt.uint32
U8 = mybir.dt.uint8
FP8X4 = mybir.dt.float8_e4m3fn_x4
ALU = mybir.AluOpType
ACTF = mybir.ActivationFunctionType
ET = mybir.EngineType

P = 128
FLOPS = 2 * 32 * 512 * 512 * 128

PI_F32 = 3.1415927410125732

NODES = 32
GROUPS = (2, 2, 4, 4, 4, 4, 4, 4, 4)
STARTS = (0, 2, 4, 8, 12, 16, 20, 24, 28)


def tile_polnormal_nolayer_kernel(tc, x, coords_x, coords_y, phis, dists_param, sigma_param, out):
    nc = tc.nc
    V = nc.vector
    S = nc.scalar
    T = nc.tensor
    with ExitStack() as ctx:
        const = ctx.enter_context(tc.tile_pool(name="const", bufs=1))
        tmp = ctx.enter_context(tc.tile_pool(name="tmp", bufs=2))
        tqp = ctx.enter_context(tc.tile_pool(name="tqp", bufs=2))
        yp = ctx.enter_context(tc.tile_pool(name="yp", bufs=2))
        wgp = ctx.enter_context(tc.tile_pool(name="wgp", bufs=4))
        gp = ctx.enter_context(tc.tile_pool(name="gp", bufs=14))
        wp = ctx.enter_context(tc.tile_pool(name="wp", bufs=10))
        sp = ctx.enter_context(tc.tile_pool(name="sp", bufs=3))
        xgp = ctx.enter_context(tc.tile_pool(name="xgp", bufs=3))
        cp = ctx.enter_context(tc.tile_pool(name="cp", bufs=4))
        op = ctx.enter_context(tc.tile_pool(name="op", bufs=8))
        pz = ctx.enter_context(tc.psum_pool(name="pz", bufs=3))
        ptp = ctx.enter_context(tc.psum_pool(name="ptp", bufs=3))
        pacc = ctx.enter_context(tc.psum_pool(name="pacc", bufs=2))
        ctx.enter_context(nc.allow_non_contiguous_dma(reason="rows of 256 and 512 bytes"))

        pa = const.tile([P, 16], BF16)
        V.memset(pa[:].bitcast(I32), 0)
        pv = const.tile([P, 32], BF16)
        V.memset(pv[:].bitcast(I32), 0)
        cn = const.tile([P, 512], BF16)
        nc.sync.dma_start(out=pa[0:1, :], in_=phis.unsqueeze(0))
        nc.sync.dma_start(out=pv[0:1, 0:16], in_=dists_param.unsqueeze(0))
        nc.sync.dma_start(out=pv[0:1, 16:18], in_=sigma_param.unsqueeze(0))
        nc.sync.dma_start(out=cn[0:32, :], in_=coords_x.rearrange("a o i j -> (a o) (i j)"))
        nc.sync.dma_start(out=cn[32:64, :], in_=coords_y.rearrange("a o i j -> (a o) (i j)"))
        V.memset(cn[64:128, :].bitcast(I32), 0)
        ones = const.tile([P, P], BF16)
        V.memset(ones[:], 1.0)
        xr = const.tile([P, 4, 32, 128], BF16)
        for grp in range(len(GROUPS)):
            nodes = slice(STARTS[grp], STARTS[grp] + GROUPS[grp])
            for b in range(4):
                nc.sync.dma_start(
                    out=xr[:, b, nodes, :],
                    in_=x[b].rearrange("(o q t) a v c -> q o (t a v c)", o=32, q=P, t=4)[:, nodes, :],
                )

        ident = const.tile([P, P], F32)
        make_identity(nc, ident[:])
        identb = const.tile([P, P], BF16)
        make_identity(nc, identb[:])
        identp = const.tile([P, P], F32)
        V.tensor_copy(out=identp[:].rearrange("k (p h) -> k p h", h=8), in_=ident[:].rearrange("k (h p) -> k p h", p=16))

        ctx.enter_context(tc.manual_schedule(engines={ET.PE, ET.Activation, ET.DVE}))
        warm = const.tile([P, 1], F32)
        V.memset(warm[:], 0.0)
        S.activation(out=warm[:], in_=warm[:], func=ACTF.Silu)
        pp = ptp.tile([P, 16], F32, tag="tp")
        T.matmul(out=pp[:], lhsT=ones[:], rhs=pa[:], start=True, stop=True)
        pq = pacc.tile([P, 32], F32, tag="acc")
        T.matmul(out=pq[:], lhsT=ones[:], rhs=pv[:], start=True, stop=True)
        turn = 2.0 * math.pi
        qi = const.tile([P, 2, 16], I32)
        V.tensor_scalar(out=qi[:, 0, :], in0=pp[:], scalar1=1.0 / turn, scalar2=None, op0=ALU.mult)
        V.tensor_scalar(out=qi[:, 1, :], in0=pp[:], scalar1=1.0 / turn, scalar2=0.25, op0=ALU.mult, op1=ALU.add)
        th = const.tile([P, 18], F32)
        S.activation(out=th[:], in_=pq[:, 0:18], func=ACTF.Tanh, scale=0.5)
        pc = ptp.tile([P, 4, P], BF16, tag="tp")
        cells = cn[:].rearrange("r (q t) -> r t q", t=4)
        for t in range(4):
            T.transpose(out=pc[:, t, :], in_=cells[:, t, :], identity=identb[:])
        pcv = pc[:, :, 0:64].rearrange("q t (a o) -> q a t o", a=2)
        p2 = const.tile([P, 2, 16], F32)
        for row in range(2):
            V.scalar_tensor_tensor(
                out=p2[:, row, :], in0=qi[:, row, :], scalar=-turn, in1=pp[:], op0=ALU.mult, op1=ALU.add
            )
        ang = const.tile([P, 2, 16], F32)
        V.tensor_scalar(out=ang[:, 0, :], in0=p2[:, 0, :], scalar1=-PI_F32, scalar2=PI_F32, op0=ALU.max, op1=ALU.min)
        V.tensor_scalar(out=ang[:, 1, :], in0=p2[:, 1, :], scalar1=0.5 * math.pi, scalar2=PI_F32, op0=ALU.add, op1=ALU.min)
        cs = const.tile([P, 2, 16], F32)
        S.activation(out=cs[:], in_=ang[:], func=ACTF.Sin)
        cq = const.tile([P, 2, 4, 32], F32)
        V.tensor_copy(out=cq[:], in_=pcv)
        sq = const.tile([P, 2, 4, 32], F32)
        S.activation(out=sq[:], in_=cq[:], func=ACTF.Square)
        warm_exp = const.tile([P, 1], F32)
        S.activation(out=warm_exp[:], in_=warm[:], func=ACTF.Exp)
        dm2 = const.tile([P, 16], F32)
        V.tensor_scalar(out=dm2[:], in0=th[:, 0:16], scalar1=1.0, scalar2=-2.0, op0=ALU.add, op1=ALU.mult)
        dd = const.tile([P, 16], F32)
        V.tensor_scalar(out=dd[:], in0=th[:, 0:16], scalar1=1.0, scalar2=None, op0=ALU.add)
        dsq = const.tile([P, 16], F32)
        V.tensor_tensor(out=dsq[:], in0=dd[:], in1=dd[:], op=ALU.mult)
        r2q = const.tile([P, 4, 32], F32)
        sg = const.tile([P, 2], F32)
        sgm = const.tile([P, 2], F32)
        nha = const.tile([P, 2], F32)

        tqs = {}
        yts = {}

        tparts = {}

        def table_part(grp, part):
            size = GROUPS[grp]
            nodes = slice(STARTS[grp], STARTS[grp] + size)
            shape = [P, size, 4, 16]
            if part < 2:
                prod = tmp.tile(shape, F32, name="prod%d" % part)
                V.tensor_tensor(
                    out=prod[:],
                    in0=cq[:, part, :, nodes].rearrange("q t o -> q o t").unsqueeze(3).to_broadcast(shape),
                    in1=cs[:, 1 - part, :].unsqueeze(1).unsqueeze(1).to_broadcast(shape),
                    op=ALU.mult,
                )
                tparts[(grp, part)] = prod
            else:
                tq = tqp.tile(shape, F32, name="tq")
                V.tensor_tensor(out=tq[:], in0=tparts[(grp, 0)][:], in1=tparts[(grp, 1)][:], op=ALU.add)
                tqs[grp] = tq
                y = yp.tile([P, size, 4, 2, 8, 16], F32, name="y")
                yts[grp] = y

        def stage_y(grp, l, h):
            d = 2 * h + l
            V.tensor_scalar(
                out=yts[grp][:, :, :, l, h, :], in0=tqs[grp][:], scalar1=dm2[:, d : d + 1], scalar2=dsq[:, d : d + 1],
                op0=ALU.mult, op1=ALU.add,
            )

        xc = const.tile([P, 4096], U32, align_bytes=64)
        xs = const.tile([P, 4096], U8, align_bytes=64)
        xgs = {}

        def x_copy(grp, b):
            size = GROUPS[grp]
            if b == 0:
                xg_new = xgp.tile([P, size, 4, 32, 4], BF16, align_bytes=64, name="xg")
                xgs[grp] = xg_new
            V.tensor_copy(
                out=xgs[grp][:, :, b, :, :].rearrange("q o (k i) t -> q o k t i", i=4),
                in_=xr[:, b, STARTS[grp] : STARTS[grp] + size, :].rearrange("q o (t k i) -> q o k t i", t=4, i=4),
            )

        def x_quant(grp, first, size):
            o = STARTS[grp] + first
            cols = slice(128 * o, 128 * (o + size))
            V.quantize_mx(
                out=xc[:, cols].bitcast(FP8X4), scales=xs[:, cols],
                in_=xgs[grp][:, first : first + size].rearrange("q o b c t -> q (o b c t)"),
            )

        zs = {}
        gs = {}
        sums = {}
        ws = {}
        tbs = {}
        wgs = {}
        accs = {}
        codes = {}
        tots = {}
        invs = {}

        def group_of(o):
            grp = max(g for g in range(len(GROUPS)) if STARTS[g] <= o)
            return grp, o - STARTS[grp]

        def stage_z(o, ls):
            grp, n = group_of(o)
            for l in ls:
                zb = pz.tile([P, 4, P], F32, tag="zb")
                for t in range(4):
                    T.matmul(
                        out=zb[:, t, :], lhsT=r2q[:, t, o : o + 1].to_broadcast([P, P]), rhs=ident[:], is_transpose=True,
                        start=True, stop=False,
                    )
                    T.matmul(
                        out=zb[:, t, :], lhsT=yts[grp][:, n, t, l].rearrange("q h p -> q (h p)"), rhs=ident[:],
                        is_transpose=True, start=False, stop=True,
                    )
                zs[(o, l)] = zb

        def stage_e(o, l):
            if l == 0 and o % 2 == 0:
                ssum_new = sp.tile([P, 8], F32, name="ssum")
                sums[o] = ssum_new
                sums[o + 1] = ssum_new
            for s in range(2):
                g = gp.tile([P, 512], F32)
                c = 4 * (o % 2) + 2 * l + s
                S.activation(
                    out=g[:].rearrange("m (u q e) -> m u q e", u=2, e=2),
                    in_=zs[(o, l)][:].rearrange("m (u e) q -> m u q e", e=2),
                    func=ACTF.Exp,
                    scale=nha[:, s : s + 1],
                    accum_out=sums[o][:, c : c + 1],
                )
                gs[(o, l, s)] = g

        def stage_tot(parts):
            first = 4 * (parts[0][0] % 2) + 2 * parts[0][1]
            tot = sp.tile([P, 2 * len(parts)], F32)
            V.tensor_scalar(
                out=tot[:], in0=sums[parts[0][0]][:, first : first + 2 * len(parts)], scalar1=1e-20, scalar2=None,
                op0=ALU.add,
            )
            tots[parts] = tot

        def stage_inv(parts):
            inv = sp.tile([P, 2 * len(parts)], F32)
            V.reciprocal(out=inv[:], in_=tots[parts][:])
            for c in range(2 * len(parts)):
                o, l = parts[c // 2]
                invs[(o, l, c % 2)] = inv[:, c : c + 1]

        def stage_n(o, ls):
            for l in ls:
                for s in range(2):
                    w = wp.tile([P, 512], BF16)
                    V.tensor_scalar(
                        out=w[:], in0=gs[(o, l, s)][:], scalar1=invs[(o, l, s)], scalar2=None, op0=ALU.mult
                    )
                    ws[(o, l, s)] = w

        def stage_w(o, ls, pool):
            for l in ls:
                if pool is ptp:
                    tb = ptp.tile([P, 2, 2, P], F32, tag="tp")
                else:
                    tb = pz.tile([P, 2, 2, P], F32, tag="zb")
                for s in range(2):
                    words = ws[(o, l, s)][:].bitcast(F32)
                    for u in range(2):
                        T.transpose(out=tb[:, s, u, :], in_=words[:, P * u : P * u + P], identity=identp[:])
                tbs[(o, l)] = tb

        def stage_c(o, ls):
            if o not in wgs:
                wg = wgp.tile([P, 2048], BF16, align_bytes=64)
                wgs[o] = wg
            wv = wgs[o][:].bitcast(F32).rearrange("q (i n u) -> q i n u", i=4, u=2)
            for l in ls:
                S.copy(out=wv[:, 2 * l : 2 * l + 2], in_=tbs[(o, l)][:].rearrange("q s u n -> q s n u"))

        def node_q(o, ls):
            first, last = 2 * ls[0], 2 * ls[-1] + 2
            cols = slice(P * first, P * last)
            wc = cp.tile([P, 512], U32, align_bytes=64)
            wsc = cp.tile([P, 512], U8, align_bytes=64)
            V.quantize_mx(
                out=wc[:, cols].bitcast(FP8X4), scales=wsc[:, cols], in_=wgs[o][:, 512 * first : 512 * last]
            )
            codes[(o, ls)] = (wc, wsc)

        def node_m(o, ls, pool):
            wc, wsc = codes[(o, ls)]
            acc = pool.tile([P, 512], F32, tag="zb" if pool is pz else "tp" if pool is ptp else "acc")
            for i in range(2 * ls[0], 2 * ls[-1] + 2):
                mc = slice(P * i, P * i + P)
                oc = slice(P * o, P * o + P)
                T.matmul_mx(
                    out=acc[:, mc],
                    lhsT=wc[:, mc].bitcast(FP8X4),
                    lhsT_scale=wsc[:, mc],
                    rhs=xc[:, oc].bitcast(FP8X4),
                    rhs_scale=xs[:, oc],
                    start=True,
                    stop=True,
                )
            accs[(o, ls)] = acc

        def node_o(o, ls, on_scalar):
            osb = op.tile([P, 4, 2 * len(ls), 32], F32)
            src = accs[(o, ls)][:, 256 * ls[0] : 256 * ls[-1] + 256].rearrange("q (i b c) -> q b i c", b=4, c=32)
            if on_scalar:
                S.copy(out=osb[:], in_=src)
            else:
                V.tensor_copy(out=osb[:], in_=src)
            dst = out[:, o, 0].rearrange("b p (h l) s c -> (p h) b l (s c)", l=2)
            if len(ls) == 2:
                dst = dst.rearrange("m b l k -> m b (l k)")
            else:
                dst = dst[:, :, ls[0], :]
            nc.sync.dma_start(out=dst, in_=osb[:].rearrange("q b i c -> q b (i c)"))

        jobs = {}

        def job(step, fn, *args):
            jobs.setdefault(max(step, 0), []).append((fn, args))

        for grp in range(1, len(GROUPS)):
            steps = GROUPS[grp - 1]
            first = STARTS[grp] - 1 - steps
            for part in range(3):
                job(first - 3 + part, table_part, grp, part)
            for k in range(16):
                job(first + k * steps // 16, stage_y, grp, k // 8, k % 8)
        for grp in range(len(GROUPS)):
            size = GROUPS[grp]
            for b in range(4):
                job(STARTS[grp] + 3 - size + b * size // 4, x_copy, grp, b)
            for n in range(0, size, 4):
                job(STARTS[grp] + 3 + n // 2, x_quant, grp, n, min(size, 4))

        both = (0, 1)
        last = NODES - 1
        for part in range(3):
            table_part(0, part)
        V.tensor_tensor(out=r2q[:], in0=sq[:, 0], in1=sq[:, 1], op=ALU.add)
        for h in range(8):
            stage_y(0, 0, h)
            if h == 1:
                V.tensor_scalar(out=sg[:], in0=th[:, 16:18], scalar1=1.0, scalar2=1e-10, op0=ALU.add, op1=ALU.max)
            if h == 4:
                V.scalar_tensor_tensor(out=sgm[:], in0=sg[:], scalar=-2.0, in1=sg[:], op0=ALU.mult, op1=ALU.mult)
        stage_z(0, (0,))
        V.reciprocal(out=nha[:], in_=sgm[:])
        for h in range(8):
            stage_y(0, 1, h)
        stage_z(0, (1,))
        for j in range(NODES):
            fill = list(jobs.get(j, []))

            def take(count):
                for i in range(count):
                    if fill:
                        fn, args = fill.pop(0)
                        fn(*args)

            stage_e(j, 0)
            stage_e(j, 1)
            if j >= 3:
                stage_c(j - 3, both)
            if j >= 7 and j % 2 == 1:
                node_o(j - 6, both, j % 8 == 7 or j < 10)
            if j < last:
                stage_z(j + 1, (0,))
            if j >= 6 and j % 2 == 0:
                node_m(j - 6, both, pacc)
                node_m(j - 5, both, pacc)
            if j < last:
                stage_z(j + 1, (1,))
            if j >= 2:
                if j % 2 == 0:
                    pair = ((j - 2, 0), (j - 2, 1), (j - 1, 0), (j - 1, 1))
                    stage_tot(pair)
                    take(2)
                    stage_inv(pair)
                    take(2)
                stage_n(j - 2, both)
                stage_w(j - 2, both, ptp)
            if j == last:
                stage_tot(((last - 1, 0), (last - 1, 1)))
            if j >= 4:
                node_q(j - 4, both)
            if j == last:
                stage_inv(((last - 1, 0), (last - 1, 1)))
            if j >= 7 and j % 2 == 1:
                node_o(j - 7, both, False)
            take(len(fill))
        node_m(last - 5, both, pacc)
        node_m(last - 4, both, pacc)
        stage_n(last - 1, (0,))
        stage_w(last - 1, (0,), pz)
        stage_tot(((last, 0),))
        stage_n(last - 1, (1,))
        stage_w(last - 1, (1,), pz)
        stage_inv(((last, 0),))
        stage_c(last - 2, both)
        node_o(last - 4, both, True)
        node_q(last - 3, both)
        stage_tot(((last, 1),))
        stage_n(last, (0,))
        stage_w(last, (0,), pz)
        node_m(last - 3, both, ptp)
        stage_inv(((last, 1),))
        node_o(last - 5, both, False)
        stage_n(last, (1,))
        stage_w(last, (1,), ptp)
        stage_c(last - 1, both)
        node_q(last - 2, both)
        node_m(last - 2, both, ptp)
        stage_c(last, (0,))
        node_q(last - 1, both)
        node_m(last - 1, both, pz)
        stage_c(last, (1,))
        for l in both:
            node_q(last, (l,))
            node_m(last, (l,), pz)
        node_o(last - 3, both, True)
        node_o(last - 2, both, True)
        node_o(last - 1, both, False)
        node_o(last, (0,), True)
        node_o(last, (1,), False)
